import numpy as np
import ml_dtypes


def mxq(x, axis, fmt="e4m3"):
    dtype, down = {"e4m3": (ml_dtypes.float8_e4m3fn, 7), "e5m2": (ml_dtypes.float8_e5m2, 14)}[fmt]
    v = np.moveaxis(np.asarray(x, np.float32).astype(ml_dtypes.bfloat16).astype(np.float64), axis, -1)
    blocks = v.reshape(v.shape[:-1] + (-1, 32))
    amax = np.abs(blocks).max(-1, keepdims=True)
    byte = np.maximum(np.where(amax > 0, np.frexp(amax)[1] - 1 + 127, 0) - down, 1)
    scale = np.exp2(byte - 127.0)
    codes = (blocks / scale).astype(np.float32).astype(dtype).astype(np.float64)
    return np.moveaxis((codes * scale).reshape(v.shape), -1, axis)


WIDE = False


def mx_kscale(k):
    if not WIDE:
        return np.ones(k)
    levels = np.array([10, -10, 5, -5, 0])
    a = np.random.permutation(np.resize(levels, k // 512 * 4)).reshape(k // 512, 4)
    idx = np.arange(k)
    return np.exp2(a[idx // 512, idx % 128 // 32])


BF16 = ml_dtypes.bfloat16


def bf(x):
    return np.asarray(x, np.float32).astype(BF16)


def f64(x):
    return np.asarray(x).astype(np.float64)


E2M1 = np.array([0.0, 0.5, 1.0, 1.5, 2.0, 3.0, 4.0, 6.0, -0.0, -0.5, -1.0, -1.5, -2.0, -3.0, -4.0, -6.0])


def pack_weight(w, fmt):
    k, n = w.shape
    w = f64(bf(w)).reshape(k // 32, 32, n)
    amax = np.abs(w).max(1)
    if fmt == "e4m3":
        byte = np.frexp(amax)[1] - 1 + 127 - 7
    else:
        mant, ex = np.frexp(amax / 6.0)
        byte = np.where(mant > 0.5, ex, ex - 1) + 127
    byte = np.clip(np.where(amax > 0, byte, 1), 1, 254)
    scaled = (w * np.exp2(127.0 - byte)[:, None, :]).reshape(k, n).astype(np.float32)
    by_word = np.ascontiguousarray(scaled.reshape(k // 512, 128, 4, n).transpose(0, 1, 3, 2))
    if fmt == "e4m3":
        words = by_word.astype(ml_dtypes.float8_e4m3fn).view(np.uint8)
    else:
        c = by_word.astype(ml_dtypes.float4_e2m1fn).view(np.uint8) & 0xF
        words = c[..., 0::2] | (c[..., 1::2] << 4)
    return np.ascontiguousarray(words), np.ascontiguousarray(byte.astype(np.uint8).reshape(k // 512, 16, n))


def unpack_weight(words, scales, fmt):
    g, p, n, _ = words.shape
    if fmt == "e4m3":
        vals = np.ascontiguousarray(words).view(ml_dtypes.float8_e4m3fn).astype(np.float64)
    else:
        nib = np.empty((g, p, n, 4), np.uint8)
        nib[..., 0::2] = words & 0xF
        nib[..., 1::2] = words >> 4
        vals = E2M1[nib]
    vals = vals * np.repeat(np.exp2(scales.astype(np.float64) - 127.0), 8, axis=1)[..., None]
    return vals.transpose(0, 1, 3, 2).reshape(g * 512, n)


B, STOCH, ACT_DIM, HIDDEN, DETER = 256, 1024, 512, 2048, 2048
K1 = STOCH + ACT_DIM
EPS = 1e-4
FMT = "e4m3"


def silu(v):
    return v / (1.0 + np.exp(-v))


def rmsnorm(v, w):
    return v * (1.0 / np.sqrt(np.mean(v * v, axis=-1, keepdims=True) + EPS)) * w


def setup_inputs():
    s = mx_kscale(K1)[:STOCH]
    w1 = np.random.standard_normal((HIDDEN, K1)) * 0.07 / np.sqrt(K1)
    w1[:, :STOCH] = w1[:, :STOCH] / s
    stoch = bf(np.random.standard_normal((B, STOCH)) * s)
    action = bf(np.random.standard_normal((B, ACT_DIM)))
    w1_words, w1_scales = pack_weight(np.ascontiguousarray(w1.T), FMT)
    tok_b1 = bf(np.random.standard_normal(HIDDEN) * 0.03)
    tok_nw = bf(1.0 + 0.1 * np.random.standard_normal(HIDDEN))
    w2 = np.random.standard_normal((DETER, HIDDEN)) * 1.5 / np.sqrt(HIDDEN)
    w2_words, w2_scales = pack_weight(np.ascontiguousarray(w2.T), FMT)
    tok_b2 = bf(np.random.standard_normal(DETER) * 0.2)
    return {"stoch": stoch,
            "action": action,
            "tok_w1_words": w1_words,
            "tok_w1_scales": w1_scales,
            "tok_b1": tok_b1,
            "tok_nw": tok_nw,
            "tok_w2_words": w2_words,
            "tok_w2_scales": w2_scales,
            "tok_b2": tok_b2}


def reference(stoch, action, tok_w1_words, tok_w1_scales, tok_b1, tok_nw, tok_w2_words, tok_w2_scales, tok_b2):
    act = f64(action)
    act = act / np.maximum(np.abs(act), 1.0)
    u = np.concatenate([f64(stoch), act], axis=-1)
    h = (mxq(u, 1, "e4m3") @ unpack_weight(tok_w1_words, tok_w1_scales, FMT)) + f64(tok_b1)
    g = silu(rmsnorm(h, f64(tok_nw)))
    return (mxq(g, 1, "e4m3") @ unpack_weight(tok_w2_words, tok_w2_scales, FMT)) + f64(tok_b2)

@@ -1,0 +1,238 @@
+from contextlib import ExitStack
+
+import concourse.mybir as mybir
+from concourse.masks import make_identity
+
+F32 = mybir.dt.float32
+BF16 = mybir.dt.bfloat16
+I32 = mybir.dt.int32
+U32 = mybir.dt.uint32
+U8 = mybir.dt.uint8
+FP8X4 = mybir.dt.float8_e4m3fn_x4
+ALU = mybir.AluOpType
+ACT = mybir.ActivationFunctionType
+
+P = 128
+PACK = 4
+K_PASS = P * PACK
+BANK = 512
+
+BATCH, STOCH, ACTION, HIDDEN, DETER = 256, 1024, 512, 2048, 2048
+K1 = STOCH + ACTION
+ROW_TILES = BATCH // P
+PASSES1 = K1 // K_PASS
+PASSES2 = HIDDEN // K_PASS
+CHUNKS1 = HIDDEN // BANK
+CHUNKS2 = DETER // BANK
+EPS = 1e-4
+LAG = 2
+
+FLOPS = 2 * BATCH * (K1 * HIDDEN + HIDDEN * DETER)
+
+
+def tile_mamba2backbone_pa_kernel(
+    tc, stoch, action, tok_w1_words, tok_w1_scales, tok_b1, tok_nw, tok_w2_words, tok_w2_scales, tok_b2, out
+):
+    nc = tc.nc
+    with ExitStack() as ctx:
+        keep = ctx.enter_context(tc.tile_pool(name="keep", bufs=1))
+        stage = ctx.enter_context(tc.tile_pool(name="stage", bufs=3))
+        psum = ctx.enter_context(tc.psum_pool(name="psum", bufs=8))
+
+        w1_planes = keep.tile([P, HIDDEN], U8, align_bytes=64)
+        w2_planes = keep.tile([P, DETER], U8, align_bytes=64)
+        vec_rows = keep.tile([P, BANK], BF16)
+        neg_half = keep.tile([P, 1], F32)
+        warm = keep.tile([P, 1], F32)
+        nc.vector.memset(vec_rows[:].bitcast(I32), 0)
+        nc.vector.memset(w1_planes[:].bitcast(I32), 0)
+        nc.vector.memset(w2_planes[:].bitcast(I32), 0)
+        nc.vector.memset(neg_half[:], -0.5)
+        for i, vec in enumerate((tok_b1, tok_nw)):
+            nc.scalar.dma_start(out=vec_rows[i:P:32, :], in_=vec.rearrange("(c n) -> c n", n=BANK))
+        nc.scalar.activation(out=warm[:], in_=neg_half[:], func=ACT.Silu)
+        ident_bf = keep.tile([P, P], BF16)
+        ident_f32 = keep.tile([P, P], F32)
+        make_identity(nc, ident_bf[:])
+        make_identity(nc, ident_f32[:])
+
+        u_rows = [keep.tile([P, K1], BF16, name="u_rows%d" % m) for m in range(ROW_TILES)]
+        for m in range(ROW_TILES):
+            nc.sync.dma_start(out=u_rows[m][:, 0:STOCH], in_=stoch[m * P : (m + 1) * P, :])
+        for m in range(ROW_TILES):
+            nc.sync.dma_start(out=u_rows[m][:, STOCH:K1], in_=action[m * P : (m + 1) * P, :])
+        for q in range(4):
+            nc.sync.dma_start(
+                out=w1_planes[32 * q : 32 * q + 4 * PASSES1, :].bitcast(I32),
+                in_=tok_w1_scales[:, 4 * q : 4 * q + 4, :].bitcast(I32),
+            )
+        w1_words = keep.tile([P, PASSES1, HIDDEN], U32, align_bytes=64)
+        w1_dram = tok_w1_words.rearrange("g p n t -> p g (n t)")
+        for c in range(CHUNKS1):
+            nc.sync.dma_start(
+                out=w1_words[:, :, c * BANK : (c + 1) * BANK].bitcast(I32),
+                in_=w1_dram[:, :, c * BANK * PACK : (c + 1) * BANK * PACK].bitcast(I32),
+            )
+        for q in range(4):
+            nc.sync.dma_start(
+                out=w2_planes[32 * q : 32 * q + 4 * PASSES2, :].bitcast(I32),
+                in_=tok_w2_scales[:, 4 * q : 4 * q + 4, :].bitcast(I32),
+            )
+        w2_words = keep.tile([P, PASSES2, DETER], U32, align_bytes=64)
+        for g in range(PASSES2):
+            nc.sync.dma_start(
+                out=w2_words[:, g, :].bitcast(I32),
+                in_=tok_w2_words[g].rearrange("p n t -> p (n t)").bitcast(I32),
+            )
+        b2_all = keep.tile([P, DETER], BF16)
+        nc.sync.dma_start(out=b2_all[:], in_=tok_b2.partition_broadcast(P))
+
+        vec_sorted = keep.tile([P, BANK], BF16)
+        nc.vector.tensor_copy(
+            out=vec_sorted[:].rearrange("q (t p) -> q t p", t=PACK), in_=vec_rows[:].rearrange("q (p t) -> q t p", t=PACK)
+        )
+
+        def spread(i, rows, dest):
+            for half in range(2):
+                bank = psum.tile([P, 2, BANK], BF16, tag="bank", name="spread_bank")
+                for j in range(2):
+                    c = 2 * half + j
+                    nc.tensor.matmul(
+                        out=bank[:, j, :],
+                        lhsT=ident_bf[:, 32 * c + i : 32 * c + i + 1].to_broadcast([P, P]),
+                        rhs=rows[:],
+                        start=True,
+                        stop=True,
+                    )
+                nc.scalar.copy(
+                    out=dest[:, 2 * half * BANK : 2 * (half + 1) * BANK], in_=bank[:].rearrange("q j n -> q (j n)")
+                )
+
+        b1_all = keep.tile([P, HIDDEN], BF16)
+        nw_all = keep.tile([P, HIDDEN], BF16)
+        spread(0, vec_sorted, b1_all)
+
+        for m in range(ROW_TILES):
+            nc.vector.tensor_scalar(
+                out=u_rows[m][:, STOCH:K1], in0=u_rows[m][:, STOCH:K1], scalar1=-1.0, scalar2=1.0, op0=ALU.max, op1=ALU.min
+            )
+        u_codes = keep.tile([P, PASSES1, BATCH], U32, align_bytes=64)
+        u_scales = keep.tile([P, PASSES1, BATCH], U8, align_bytes=64)
+        for g in range(PASSES1):
+            ut = psum.tile([P, ROW_TILES, 2, P], F32, tag="bank", name="ut")
+            for m in range(ROW_TILES):
+                words = u_rows[m][:].bitcast(F32)
+                for w in range(2):
+                    nc.tensor.transpose(
+                        out=ut[:, m, w, :], in_=words[:, 256 * g + w : 256 * (g + 1) : 2], identity=ident_f32[:]
+                    )
+            u_grouped = stage.tile([P, BATCH * PACK], BF16, align_bytes=64)
+            nc.vector.tensor_copy(
+                out=u_grouped[:].bitcast(F32).rearrange("p (m b w) -> p m b w", m=ROW_TILES, w=2),
+                in_=ut[:].rearrange("p m w b -> p m b w"),
+            )
+            nc.vector.quantize_mx(out=u_codes[:, g, :].bitcast(FP8X4), scales=u_scales[:, g, :], in_=u_grouped[:])
+
+        spread(1, vec_sorted, nw_all)
+
+        hb = [keep.tile([P, HIDDEN], F32, name="hb%d" % m) for m in range(ROW_TILES)]
+        squares = keep.tile([P, ROW_TILES, HIDDEN], BF16)
+        sumsq = [keep.tile([P, CHUNKS1], F32, name="sumsq%d" % m) for m in range(ROW_TILES)]
+
+        def layer1(m, c):
+            cols = slice(c * BANK, (c + 1) * BANK)
+            acc = psum.tile([P, BANK], F32, tag="bank", name="acc1")
+            for g in range(PASSES1):
+                nc.tensor.matmul_mx(
+                    out=acc[:],
+                    lhsT=u_codes[:, g, m * P : (m + 1) * P].bitcast(FP8X4),
+                    lhsT_scale=u_scales[:, g, m * P : (m + 1) * P],
+                    rhs=w1_words[:, g, cols].bitcast(FP8X4),
+                    rhs_scale=w1_planes[4 * g : P, cols],
+                    start=(g == 0),
+                    stop=(g == PASSES1 - 1),
+                )
+            nc.vector.tensor_tensor(
+                out=hb[m][:, cols].rearrange("q (t p) -> q t p", t=PACK),
+                in0=acc[:].rearrange("q (p t) -> q t p", t=PACK),
+                in1=b1_all[:, cols].rearrange("q (t p) -> q t p", t=PACK),
+                op=ALU.add,
+            )
+            nc.scalar.activation(
+                out=squares[:, m, cols], in_=hb[m][:, cols], func=ACT.Square, accum_out=sumsq[m][:, c : c + 1]
+            )
+
+        for step in range(CHUNKS1 + LAG):
+            if step < CHUNKS1:
+                layer1(0, step)
+            if step >= LAG:
+                layer1(1, step - LAG)
+
+        g_codes = [keep.tile([P, PASSES2, P], U32, align_bytes=64, name="g_codes%d" % m) for m in range(ROW_TILES)]
+        g_scales = [keep.tile([P, PASSES2, P], U8, align_bytes=64, name="g_scales%d" % m) for m in range(ROW_TILES)]
+
+        def activations(m):
+            parts = stage.tile([P, CHUNKS1], F32, name="parts")
+            mean_eps = stage.tile([P, 1], F32, name="mean_eps")
+            rstd = stage.tile([P, 1], F32, name="rstd")
+            nc.vector.tensor_scalar(
+                out=parts[:], in0=sumsq[m][:], scalar1=1.0 / HIDDEN, scalar2=EPS, op0=ALU.mult, op1=ALU.add,
+                accum_out=mean_eps[:],
+            )
+            nc.gpsimd.tensor_tensor(out=rstd[:], in0=mean_eps[:], in1=neg_half[:], op=ALU.pow)
+            grouped = []
+            for g in range(PASSES2):
+                cols = slice(g * K_PASS, (g + 1) * K_PASS)
+                hv = stage.tile([P, K_PASS], F32, name="hv")
+                nc.vector.scalar_tensor_tensor(
+                    out=hv[:], in0=hb[m][:, cols], scalar=rstd[:, 0:1], in1=nw_all[:, cols], op0=ALU.mult, op1=ALU.mult
+                )
+                gt = psum.tile([P, PACK, P], F32, tag="bank", name="gt")
+                for t in range(PACK):
+                    nc.tensor.transpose(out=gt[:, t, :], in_=hv[:, t * P : (t + 1) * P], identity=ident_f32[:])
+                g_grouped = stage.tile([P, P * PACK], BF16, align_bytes=64, name="g_grouped", bufs=4)
+                nc.scalar.activation(
+                    out=g_grouped[:].rearrange("p (b t) -> p b t", t=PACK),
+                    in_=gt[:].rearrange("p t b -> p b t"),
+                    func=ACT.Silu,
+                )
+                grouped.append(g_grouped)
+                if g > 0:
+                    quantise(m, g - 1, grouped[g - 1])
+            quantise(m, PASSES2 - 1, grouped[PASSES2 - 1])
+
+        def quantise(m, g, g_grouped):
+            nc.vector.quantize_mx(out=g_codes[m][:, g, :].bitcast(FP8X4), scales=g_scales[m][:, g, :], in_=g_grouped[:])
+
+        def pass2(acc, m, g, n):
+            cols = slice(n * BANK, (n + 1) * BANK)
+            nc.tensor.matmul_mx(
+                out=acc[:],
+                lhsT=g_codes[m][:, g, :].bitcast(FP8X4),
+                lhsT_scale=g_scales[m][:, g, :],
+                rhs=w2_words[:, g, cols].bitcast(FP8X4),
+                rhs_scale=w2_planes[4 * g : P, cols],
+                start=(g == 0),
+                stop=(g == PASSES2 - 1),
+            )
+
+        def finish(acc, m, n):
+            cols = slice(n * BANK, (n + 1) * BANK)
+            result = stage.tile([P, BANK], F32, name="result", bufs=4)
+            nc.vector.tensor_tensor(out=result[:], in0=acc[:], in1=b2_all[:, cols], op=ALU.add)
+            nc.sync.dma_start(out=out[m * P : (m + 1) * P, cols], in_=result[:])
+
+        activations(0)
+        acc0 = [psum.tile([P, BANK], F32, tag="bank", name="acc2_%d" % n) for n in range(CHUNKS2)]
+        for g in range(PASSES2):
+            if g == PASSES2 // 2:
+                activations(1)
+            for n in range(CHUNKS2):
+                pass2(acc0[n], 0, g, n)
+        for n in range(CHUNKS2):
+            finish(acc0[n], 0, n)
+        for n in range(CHUNKS2):
+            acc = psum.tile([P, BANK], F32, tag="bank", name="acc2")
+            for g in range(PASSES2):
+                pass2(acc, 1, g, n)
+            finish(acc, 1, n)

@@ -30,6 +30,14 @@ LAG = 2
 FLOPS = 2 * BATCH * (K1 * HIDDEN + HIDDEN * DETER)
 
 
+def pairs_apart(ap):
+    return ap.rearrange("q (p w e) -> q w p e", w=2, e=2)
+
+
+def by_pair(ap):
+    return ap.rearrange("q (w p e) -> q w p e", w=2, e=2)
+
+
 def tile_mamba2backbone_pa_kernel(
     tc, stoch, action, tok_w1_words, tok_w1_scales, tok_b1, tok_nw, tok_w2_words, tok_w2_scales, tok_b2, out
 ):
@@ -88,9 +96,7 @@ def tile_mamba2backbone_pa_kernel(
         nc.sync.dma_start(out=b2_all[:], in_=tok_b2.partition_broadcast(P))
 
         vec_sorted = keep.tile([P, BANK], BF16)
-        nc.vector.tensor_copy(
-            out=vec_sorted[:].rearrange("q (t p) -> q t p", t=PACK), in_=vec_rows[:].rearrange("q (p t) -> q t p", t=PACK)
-        )
+        nc.vector.tensor_copy(out=by_pair(vec_sorted[:]), in_=pairs_apart(vec_rows[:]))
 
         def spread(i, rows, dest):
             for half in range(2):
@@ -153,10 +159,7 @@ def tile_mamba2backbone_pa_kernel(
                     stop=(g == PASSES1 - 1),
                 )
             nc.vector.tensor_tensor(
-                out=hb[m][:, cols].rearrange("q (t p) -> q t p", t=PACK),
-                in0=acc[:].rearrange("q (p t) -> q t p", t=PACK),
-                in1=b1_all[:, cols].rearrange("q (t p) -> q t p", t=PACK),
-                op=ALU.add,
+                out=by_pair(hb[m][:, cols]), in0=pairs_apart(acc[:]), in1=by_pair(b1_all[:, cols]), op=ALU.add
             )
             nc.scalar.activation(
                 out=squares[:, m, cols], in_=hb[m][:, cols], func=ACT.Square, accum_out=sumsq[m][:, c : c + 1]
@@ -180,29 +183,31 @@ def tile_mamba2backbone_pa_kernel(
                 accum_out=mean_eps[:],
             )
             nc.gpsimd.tensor_tensor(out=rstd[:], in0=mean_eps[:], in1=neg_half[:], op=ALU.pow)
-            grouped = []
-            for g in range(PASSES2):
-                cols = slice(g * K_PASS, (g + 1) * K_PASS)
-                hv = stage.tile([P, K_PASS], F32, name="hv")
-                nc.vector.scalar_tensor_tensor(
-                    out=hv[:], in0=hb[m][:, cols], scalar=rstd[:, 0:1], in1=nw_all[:, cols], op0=ALU.mult, op1=ALU.mult
-                )
-                gt = psum.tile([P, PACK, P], F32, tag="bank", name="gt")
-                for t in range(PACK):
-                    nc.tensor.transpose(out=gt[:, t, :], in_=hv[:, t * P : (t + 1) * P], identity=ident_f32[:])
-                g_grouped = stage.tile([P, P * PACK], BF16, align_bytes=64, name="g_grouped", bufs=4)
-                nc.scalar.activation(
-                    out=g_grouped[:].rearrange("p (b t) -> p b t", t=PACK),
-                    in_=gt[:].rearrange("p t b -> p b t"),
-                    func=ACT.Silu,
-                )
-                grouped.append(g_grouped)
+            banks = []
+            for g in range(PASSES2 + 1):
+                if g < PASSES2:
+                    cols = slice(g * K_PASS, (g + 1) * K_PASS)
+                    hv = stage.tile([P, K_PASS], F32, name="hv")
+                    nc.vector.scalar_tensor_tensor(
+                        out=hv[:], in0=hb[m][:, cols], scalar=rstd[:, 0:1], in1=nw_all[:, cols], op0=ALU.mult, op1=ALU.mult
+                    )
+                    g_rows = stage.tile([P, K_PASS], BF16, name="g_rows")
+                    nc.scalar.activation(out=g_rows[:], in_=hv[:], func=ACT.Silu)
+                    gt = psum.tile([P, 2, P], F32, tag="bank", name="gt")
+                    for w in range(2):
+                        nc.tensor.transpose(
+                            out=gt[:, w, :], in_=g_rows[:].bitcast(F32)[:, w * P : (w + 1) * P], identity=ident_f32[:]
+                        )
+                    banks.append(gt)
                 if g > 0:
-                    quantise(m, g - 1, grouped[g - 1])
-            quantise(m, PASSES2 - 1, grouped[PASSES2 - 1])
-
-        def quantise(m, g, g_grouped):
-            nc.vector.quantize_mx(out=g_codes[m][:, g, :].bitcast(FP8X4), scales=g_scales[m][:, g, :], in_=g_grouped[:])
+                    g_grouped = stage.tile([P, P * PACK], BF16, align_bytes=64, name="g_grouped")
+                    nc.scalar.copy(
+                        out=g_grouped[:].bitcast(F32).rearrange("p (b w) -> p b w", w=2),
+                        in_=banks[g - 1][:].rearrange("p w b -> p b w"),
+                    )
+                    nc.vector.quantize_mx(
+                        out=g_codes[m][:, g - 1, :].bitcast(FP8X4), scales=g_scales[m][:, g - 1, :], in_=g_grouped[:]
+                    )
 
         def pass2(acc, m, g, n):
             cols = slice(n * BANK, (n + 1) * BANK)

@@ -30,14 +30,6 @@ LAG = 2
 FLOPS = 2 * BATCH * (K1 * HIDDEN + HIDDEN * DETER)
 
 
-def pairs_apart(ap):
-    return ap.rearrange("q (p w e) -> q w p e", w=2, e=2)
-
-
-def by_pair(ap):
-    return ap.rearrange("q (w p e) -> q w p e", w=2, e=2)
-
-
 def tile_mamba2backbone_pa_kernel(
     tc, stoch, action, tok_w1_words, tok_w1_scales, tok_b1, tok_nw, tok_w2_words, tok_w2_scales, tok_b2, out
 ):
@@ -56,7 +48,7 @@ def tile_mamba2backbone_pa_kernel(
         nc.vector.memset(w1_planes[:].bitcast(I32), 0)
         nc.vector.memset(w2_planes[:].bitcast(I32), 0)
         nc.vector.memset(neg_half[:], -0.5)
-        for i, vec in enumerate((tok_b1, tok_nw)):
+        for i, vec in enumerate((tok_b1, tok_nw, tok_b2)):
             nc.scalar.dma_start(out=vec_rows[i:P:32, :], in_=vec.rearrange("(c n) -> c n", n=BANK))
         nc.scalar.activation(out=warm[:], in_=neg_half[:], func=ACT.Silu)
         ident_bf = keep.tile([P, P], BF16)
@@ -92,11 +84,11 @@ def tile_mamba2backbone_pa_kernel(
                 out=w2_words[:, g, :].bitcast(I32),
                 in_=tok_w2_words[g].rearrange("p n t -> p (n t)").bitcast(I32),
             )
-        b2_all = keep.tile([P, DETER], BF16)
-        nc.sync.dma_start(out=b2_all[:], in_=tok_b2.partition_broadcast(P))
 
         vec_sorted = keep.tile([P, BANK], BF16)
-        nc.vector.tensor_copy(out=by_pair(vec_sorted[:]), in_=pairs_apart(vec_rows[:]))
+        nc.vector.tensor_copy(
+            out=vec_sorted[:].rearrange("q (t p) -> q t p", t=PACK), in_=vec_rows[:].rearrange("q (p t) -> q t p", t=PACK)
+        )
 
         def spread(i, rows, dest):
             for half in range(2):
@@ -116,6 +108,7 @@ def tile_mamba2backbone_pa_kernel(
 
         b1_all = keep.tile([P, HIDDEN], BF16)
         nw_all = keep.tile([P, HIDDEN], BF16)
+        b2_all = keep.tile([P, DETER], BF16)
         spread(0, vec_sorted, b1_all)
 
         for m in range(ROW_TILES):
@@ -140,6 +133,7 @@ def tile_mamba2backbone_pa_kernel(
             nc.vector.quantize_mx(out=u_codes[:, g, :].bitcast(FP8X4), scales=u_scales[:, g, :], in_=u_grouped[:])
 
         spread(1, vec_sorted, nw_all)
+        spread(2, vec_rows, b2_all)
 
         hb = [keep.tile([P, HIDDEN], F32, name="hb%d" % m) for m in range(ROW_TILES)]
         squares = keep.tile([P, ROW_TILES, HIDDEN], BF16)
@@ -159,7 +153,10 @@ def tile_mamba2backbone_pa_kernel(
                     stop=(g == PASSES1 - 1),
                 )
             nc.vector.tensor_tensor(
-                out=by_pair(hb[m][:, cols]), in0=pairs_apart(acc[:]), in1=by_pair(b1_all[:, cols]), op=ALU.add
+                out=hb[m][:, cols].rearrange("q (t p) -> q t p", t=PACK),
+                in0=acc[:].rearrange("q (p t) -> q t p", t=PACK),
+                in1=b1_all[:, cols].rearrange("q (t p) -> q t p", t=PACK),
+                op=ALU.add,
             )
             nc.scalar.activation(
                 out=squares[:, m, cols], in_=hb[m][:, cols], func=ACT.Square, accum_out=sumsq[m][:, c : c + 1]
@@ -183,31 +180,29 @@ def tile_mamba2backbone_pa_kernel(
                 accum_out=mean_eps[:],
             )
             nc.gpsimd.tensor_tensor(out=rstd[:], in0=mean_eps[:], in1=neg_half[:], op=ALU.pow)
-            banks = []
-            for g in range(PASSES2 + 1):
-                if g < PASSES2:
-                    cols = slice(g * K_PASS, (g + 1) * K_PASS)
-                    hv = stage.tile([P, K_PASS], F32, name="hv")
-                    nc.vector.scalar_tensor_tensor(
-                        out=hv[:], in0=hb[m][:, cols], scalar=rstd[:, 0:1], in1=nw_all[:, cols], op0=ALU.mult, op1=ALU.mult
-                    )
-                    g_rows = stage.tile([P, K_PASS], BF16, name="g_rows")
-                    nc.scalar.activation(out=g_rows[:], in_=hv[:], func=ACT.Silu)
-                    gt = psum.tile([P, 2, P], F32, tag="bank", name="gt")
-                    for w in range(2):
-                        nc.tensor.transpose(
-                            out=gt[:, w, :], in_=g_rows[:].bitcast(F32)[:, w * P : (w + 1) * P], identity=ident_f32[:]
-                        )
-                    banks.append(gt)
+            grouped = []
+            for g in range(PASSES2):
+                cols = slice(g * K_PASS, (g + 1) * K_PASS)
+                hv = stage.tile([P, K_PASS], F32, name="hv")
+                nc.vector.scalar_tensor_tensor(
+                    out=hv[:], in0=hb[m][:, cols], scalar=rstd[:, 0:1], in1=nw_all[:, cols], op0=ALU.mult, op1=ALU.mult
+                )
+                gt = psum.tile([P, PACK, P], F32, tag="bank", name="gt")
+                for t in range(PACK):
+                    nc.tensor.transpose(out=gt[:, t, :], in_=hv[:, t * P : (t + 1) * P], identity=ident_f32[:])
+                g_grouped = stage.tile([P, P * PACK], BF16, align_bytes=64, name="g_grouped", bufs=4)
+                nc.scalar.activation(
+                    out=g_grouped[:].rearrange("p (b t) -> p b t", t=PACK),
+                    in_=gt[:].rearrange("p t b -> p b t"),
+                    func=ACT.Silu,
+                )
+                grouped.append(g_grouped)
                 if g > 0:
-                    g_grouped = stage.tile([P, P * PACK], BF16, align_bytes=64, name="g_grouped")
-                    nc.scalar.copy(
-                        out=g_grouped[:].bitcast(F32).rearrange("p (b w) -> p b w", w=2),
-                        in_=banks[g - 1][:].rearrange("p w b -> p b w"),
-                    )
-                    nc.vector.quantize_mx(
-                        out=g_codes[m][:, g - 1, :].bitcast(FP8X4), scales=g_scales[m][:, g - 1, :], in_=g_grouped[:]
-                    )
+                    quantise(m, g - 1, grouped[g - 1])
+            quantise(m, PASSES2 - 1, grouped[PASSES2 - 1])
+
+        def quantise(m, g, g_grouped):
+            nc.vector.quantize_mx(out=g_codes[m][:, g, :].bitcast(FP8X4), scales=g_scales[m][:, g, :], in_=g_grouped[:])
 
         def pass2(acc, m, g, n):
             cols = slice(n * BANK, (n + 1) * BANK)

@@ -44,35 +44,40 @@ def tile_mamba2backbone_pa_kernel(
         vec_rows = keep.tile([P, BANK], BF16)
         neg_half = keep.tile([P, 1], F32)
         warm = keep.tile([P, 1], F32)
-        nc.vector.memset(vec_rows[:].bitcast(I32), 0)
         nc.vector.memset(w1_planes[:].bitcast(I32), 0)
+        nc.vector.memset(vec_rows[:].bitcast(I32), 0)
         nc.vector.memset(w2_planes[:].bitcast(I32), 0)
         nc.vector.memset(neg_half[:], -0.5)
-        for i, vec in enumerate((tok_b1, tok_nw, tok_b2)):
-            nc.scalar.dma_start(out=vec_rows[i:P:32, :], in_=vec.rearrange("(c n) -> c n", n=BANK))
         nc.scalar.activation(out=warm[:], in_=neg_half[:], func=ACT.Silu)
         ident_bf = keep.tile([P, P], BF16)
         ident_f32 = keep.tile([P, P], F32)
-        make_identity(nc, ident_bf[:])
         make_identity(nc, ident_f32[:])
+        make_identity(nc, ident_bf[:])
+        for i, vec in enumerate((tok_b1, tok_nw, tok_b2)):
+            nc.gpsimd.dma_start(out=vec_rows[i:P:32, :], in_=vec.rearrange("(c n) -> c n", n=BANK))
 
-        u_rows = [keep.tile([P, K1], BF16, name="u_rows%d" % m) for m in range(ROW_TILES)]
-        for m in range(ROW_TILES):
-            nc.sync.dma_start(out=u_rows[m][:, 0:STOCH], in_=stoch[m * P : (m + 1) * P, :])
-        for m in range(ROW_TILES):
-            nc.sync.dma_start(out=u_rows[m][:, STOCH:K1], in_=action[m * P : (m + 1) * P, :])
+        u_rows = [keep.tile([P, ROW_TILES, K_PASS], BF16, name="u_rows%d" % g) for g in range(PASSES1)]
+        for g in range(PASSES1):
+            k0 = g * K_PASS
+            source = stoch[:, k0 : k0 + K_PASS] if k0 < STOCH else action[:, k0 - STOCH : k0 - STOCH + K_PASS]
+            nc.sync.dma_start(out=u_rows[g][:], in_=source.rearrange("(m p) k -> p m k", p=P))
+        w1_words = keep.tile([P, PASSES1, HIDDEN], U32, align_bytes=64)
+        w1_dram = tok_w1_words.rearrange("g p n t -> p g (n t)")
+
+        def load_w1(c):
+            nc.sync.dma_start(
+                out=w1_words[:, :, c * BANK : (c + 1) * BANK].bitcast(I32),
+                in_=w1_dram[:, :, c * BANK * PACK : (c + 1) * BANK * PACK].bitcast(I32),
+            )
+
+        load_w1(0)
         for q in range(4):
             nc.sync.dma_start(
                 out=w1_planes[32 * q : 32 * q + 4 * PASSES1, :].bitcast(I32),
                 in_=tok_w1_scales[:, 4 * q : 4 * q + 4, :].bitcast(I32),
             )
-        w1_words = keep.tile([P, PASSES1, HIDDEN], U32, align_bytes=64)
-        w1_dram = tok_w1_words.rearrange("g p n t -> p g (n t)")
-        for c in range(CHUNKS1):
-            nc.sync.dma_start(
-                out=w1_words[:, :, c * BANK : (c + 1) * BANK].bitcast(I32),
-                in_=w1_dram[:, :, c * BANK * PACK : (c + 1) * BANK * PACK].bitcast(I32),
-            )
+        for c in range(1, CHUNKS1):
+            load_w1(c)
         for q in range(4):
             nc.sync.dma_start(
                 out=w2_planes[32 * q : 32 * q + 4 * PASSES2, :].bitcast(I32),
@@ -111,20 +116,16 @@ def tile_mamba2backbone_pa_kernel(
         b2_all = keep.tile([P, DETER], BF16)
         spread(0, vec_sorted, b1_all)
 
-        for m in range(ROW_TILES):
-            nc.vector.tensor_scalar(
-                out=u_rows[m][:, STOCH:K1], in0=u_rows[m][:, STOCH:K1], scalar1=-1.0, scalar2=1.0, op0=ALU.max, op1=ALU.min
-            )
+        for g in range(STOCH // K_PASS, PASSES1):
+            nc.vector.tensor_scalar(out=u_rows[g][:], in0=u_rows[g][:], scalar1=-1.0, scalar2=1.0, op0=ALU.max, op1=ALU.min)
         u_codes = keep.tile([P, PASSES1, BATCH], U32, align_bytes=64)
         u_scales = keep.tile([P, PASSES1, BATCH], U8, align_bytes=64)
         for g in range(PASSES1):
             ut = psum.tile([P, ROW_TILES, 2, P], F32, tag="bank", name="ut")
             for m in range(ROW_TILES):
-                words = u_rows[m][:].bitcast(F32)
+                words = u_rows[g][:, m, :].bitcast(F32)
                 for w in range(2):
-                    nc.tensor.transpose(
-                        out=ut[:, m, w, :], in_=words[:, 256 * g + w : 256 * (g + 1) : 2], identity=ident_f32[:]
-                    )
+                    nc.tensor.transpose(out=ut[:, m, w, :], in_=words[:, w::2], identity=ident_f32[:])
             u_grouped = stage.tile([P, BATCH * PACK], BF16, align_bytes=64)
             nc.vector.tensor_copy(
                 out=u_grouped[:].bitcast(F32).rearrange("p (m b w) -> p m b w", m=ROW_TILES, w=2),

@@ -22,10 +22,11 @@ K1 = STOCH + ACTION
 ROW_TILES = BATCH // P
 PASSES1 = K1 // K_PASS
 PASSES2 = HIDDEN // K_PASS
-CHUNKS1 = HIDDEN // BANK
+GROUPS = HIDDEN // K_PASS
+HALF = BANK // 2
 CHUNKS2 = DETER // BANK
 EPS = 1e-4
-LAG = 2
+PAIRS = 2
 
 FLOPS = 2 * BATCH * (K1 * HIDDEN + HIDDEN * DETER)
 
@@ -36,116 +37,151 @@ def tile_mamba2backbone_pa_kernel(
     nc = tc.nc
     with ExitStack() as ctx:
         keep = ctx.enter_context(tc.tile_pool(name="keep", bufs=1))
-        stage = ctx.enter_context(tc.tile_pool(name="stage", bufs=3))
+        stage = ctx.enter_context(tc.tile_pool(name="stage", bufs=4))
         psum = ctx.enter_context(tc.psum_pool(name="psum", bufs=8))
 
+        ctx.enter_context(tc.manual_schedule())
         w1_planes = keep.tile([P, HIDDEN], U8, align_bytes=64)
         w2_planes = keep.tile([P, DETER], U8, align_bytes=64)
-        vec_rows = keep.tile([P, BANK], BF16)
         neg_half = keep.tile([P, 1], F32)
         warm = keep.tile([P, 1], F32)
+        vec_rows = [keep.tile([P, BANK], BF16, name="vec_rows%d" % i) for i in range(3)]
         nc.vector.memset(w1_planes[:].bitcast(I32), 0)
-        nc.vector.memset(vec_rows[:].bitcast(I32), 0)
-        nc.vector.memset(w2_planes[:].bitcast(I32), 0)
+        nc.vector.memset(vec_rows[0][:].bitcast(I32), 0)
         nc.vector.memset(neg_half[:], -0.5)
-        nc.scalar.activation(out=warm[:], in_=neg_half[:], func=ACT.Silu)
+        nc.vector.memset(vec_rows[1][:].bitcast(I32), 0)
+        nc.vector.memset(vec_rows[2][:].bitcast(I32), 0)
+        nc.vector.memset(w2_planes[:].bitcast(I32), 0)
         ident_bf = keep.tile([P, P], BF16)
         ident_f32 = keep.tile([P, P], F32)
         make_identity(nc, ident_f32[:])
-        make_identity(nc, ident_bf[:])
-        for i, vec in enumerate((tok_b1, tok_nw, tok_b2)):
-            nc.gpsimd.dma_start(out=vec_rows[i:P:32, :], in_=vec.rearrange("(c n) -> c n", n=BANK))
 
-        u_rows = [keep.tile([P, ROW_TILES, K_PASS], BF16, name="u_rows%d" % g) for g in range(PASSES1)]
-        for g in range(PASSES1):
-            k0 = g * K_PASS
-            source = stoch[:, k0 : k0 + K_PASS] if k0 < STOCH else action[:, k0 - STOCH : k0 - STOCH + K_PASS]
-            nc.sync.dma_start(out=u_rows[g][:], in_=source.rearrange("(m p) k -> p m k", p=P))
+        def load_vector(queue, i, vec):
+            queue.dma_start(out=vec_rows[i][0:P:32, :], in_=vec.rearrange("(c n) -> c n", n=BANK))
+
+        load_vector(nc.scalar, 0, tok_b1)
+        load_vector(nc.gpsimd, 1, tok_nw)
+        make_identity(nc, ident_bf[:])
+        load_vector(nc.gpsimd, 2, tok_b2)
+        nc.scalar.activation(out=warm[:], in_=neg_half[:], func=ACT.Silu)
+
+        stoch_rows = keep.tile([P, ROW_TILES, STOCH], BF16)
+        action_rows = keep.tile([P, ROW_TILES, ACTION], BF16)
+        nc.sync.dma_start(out=stoch_rows[:], in_=stoch.rearrange("(m p) k -> p m k", p=P))
+        nc.sync.dma_start(out=action_rows[:], in_=action.rearrange("(m p) k -> p m k", p=P))
         w1_words = keep.tile([P, PASSES1, HIDDEN], U32, align_bytes=64)
         w1_dram = tok_w1_words.rearrange("g p n t -> p g (n t)")
 
-        def load_w1(c):
+        def load_w1(c0, width):
             nc.sync.dma_start(
-                out=w1_words[:, :, c * BANK : (c + 1) * BANK].bitcast(I32),
-                in_=w1_dram[:, :, c * BANK * PACK : (c + 1) * BANK * PACK].bitcast(I32),
+                out=w1_words[:, :, c0 : c0 + width].bitcast(I32),
+                in_=w1_dram[:, :, c0 * PACK : (c0 + width) * PACK].bitcast(I32),
             )
 
-        load_w1(0)
-        for q in range(4):
+        def load_w1_scales(q):
             nc.sync.dma_start(
                 out=w1_planes[32 * q : 32 * q + 4 * PASSES1, :].bitcast(I32),
                 in_=tok_w1_scales[:, 4 * q : 4 * q + 4, :].bitcast(I32),
             )
-        for c in range(1, CHUNKS1):
-            load_w1(c)
+
+        load_w1_scales(0)
+        load_w1(0, BANK)
+        for q in range(1, 4):
+            load_w1_scales(q)
+        load_w1(BANK, BANK)
+        load_w1(2 * BANK, BANK)
+        load_w1(3 * BANK, HALF)
+        load_w1(3 * BANK + HALF, HALF)
         for q in range(4):
             nc.sync.dma_start(
                 out=w2_planes[32 * q : 32 * q + 4 * PASSES2, :].bitcast(I32),
                 in_=tok_w2_scales[:, 4 * q : 4 * q + 4, :].bitcast(I32),
             )
         w2_words = keep.tile([P, PASSES2, DETER], U32, align_bytes=64)
-        for g in range(PASSES2):
+        w2_dram = tok_w2_words.rearrange("g p n t -> p g (n t)")
+        for n in range(CHUNKS2):
             nc.sync.dma_start(
-                out=w2_words[:, g, :].bitcast(I32),
-                in_=tok_w2_words[g].rearrange("p n t -> p (n t)").bitcast(I32),
+                out=w2_words[:, :, n * BANK : (n + 1) * BANK].bitcast(I32),
+                in_=w2_dram[:, :, n * BANK * PACK : (n + 1) * BANK * PACK].bitcast(I32),
             )
 
-        vec_sorted = keep.tile([P, BANK], BF16)
-        nc.vector.tensor_copy(
-            out=vec_sorted[:].rearrange("q (t p) -> q t p", t=PACK), in_=vec_rows[:].rearrange("q (p t) -> q t p", t=PACK)
-        )
+        u_codes = keep.tile([P, PASSES1, BATCH], U32, align_bytes=64)
+        u_scales = keep.tile([P, PASSES1, BATCH], U8, align_bytes=64)
+        u_grouped = [keep.tile([P, BATCH * PACK], BF16, align_bytes=64, name="u_grouped%d" % g) for g in range(PASSES1)]
 
-        def spread(i, rows, dest):
+        def u_turn(g):
+            rows, k0 = (stoch_rows, g * K_PASS) if g * K_PASS < STOCH else (action_rows, g * K_PASS - STOCH)
+            ut = psum.tile([P, ROW_TILES, PAIRS, P], F32, tag="bank", name="ut")
+            for m in range(ROW_TILES):
+                words = rows[:, m, k0 : k0 + K_PASS].bitcast(F32)
+                for w in range(PAIRS):
+                    nc.tensor.transpose(out=ut[:, m, w, :], in_=words[:, w::2], identity=ident_f32[:])
+            copy = nc.scalar.copy if g == 1 else nc.vector.tensor_copy
+            copy(
+                out=u_grouped[g][:].bitcast(F32).rearrange("p (m b w) -> p m b w", m=ROW_TILES, w=PAIRS),
+                in_=ut[:].rearrange("p m w b -> p m b w"),
+            )
+
+        def u_quantise(g):
+            nc.vector.quantize_mx(
+                out=u_codes[:, g, :].bitcast(FP8X4), scales=u_scales[:, g, :], in_=u_grouped[g][:]
+            )
+
+        nc.vector.tensor_scalar(
+            out=action_rows[:], in0=action_rows[:], scalar1=-1.0, scalar2=1.0, op0=ALU.max, op1=ALU.min
+        )
+        u_turn(0)
+        u_turn(1)
+        u_quantise(0)
+        u_turn(2)
+        u_quantise(1)
+        u_quantise(2)
+
+        def spread(rows):
+            banks = []
             for half in range(2):
                 bank = psum.tile([P, 2, BANK], BF16, tag="bank", name="spread_bank")
                 for j in range(2):
                     c = 2 * half + j
                     nc.tensor.matmul(
                         out=bank[:, j, :],
-                        lhsT=ident_bf[:, 32 * c + i : 32 * c + i + 1].to_broadcast([P, P]),
+                        lhsT=ident_bf[:, 32 * c : 32 * c + 1].to_broadcast([P, P]),
                         rhs=rows[:],
                         start=True,
                         stop=True,
                     )
-                nc.scalar.copy(
-                    out=dest[:, 2 * half * BANK : 2 * (half + 1) * BANK], in_=bank[:].rearrange("q j n -> q (j n)")
-                )
+                banks.append(bank)
+            return banks
+
+        def spread_copy(copy, banks, half, dest):
+            copy(
+                out=dest[:, 2 * half * BANK : 2 * (half + 1) * BANK], in_=banks[half][:].rearrange("q j n -> q (j n)")
+            )
 
         b1_all = keep.tile([P, HIDDEN], BF16)
         nw_all = keep.tile([P, HIDDEN], BF16)
         b2_all = keep.tile([P, DETER], BF16)
-        spread(0, vec_sorted, b1_all)
-
-        for g in range(STOCH // K_PASS, PASSES1):
-            nc.vector.tensor_scalar(out=u_rows[g][:], in0=u_rows[g][:], scalar1=-1.0, scalar2=1.0, op0=ALU.max, op1=ALU.min)
-        u_codes = keep.tile([P, PASSES1, BATCH], U32, align_bytes=64)
-        u_scales = keep.tile([P, PASSES1, BATCH], U8, align_bytes=64)
-        for g in range(PASSES1):
-            ut = psum.tile([P, ROW_TILES, 2, P], F32, tag="bank", name="ut")
-            for m in range(ROW_TILES):
-                words = u_rows[g][:, m, :].bitcast(F32)
-                for w in range(2):
-                    nc.tensor.transpose(out=ut[:, m, w, :], in_=words[:, w::2], identity=ident_f32[:])
-            u_grouped = stage.tile([P, BATCH * PACK], BF16, align_bytes=64)
-            nc.vector.tensor_copy(
-                out=u_grouped[:].bitcast(F32).rearrange("p (m b w) -> p m b w", m=ROW_TILES, w=2),
-                in_=ut[:].rearrange("p m w b -> p m b w"),
-            )
-            nc.vector.quantize_mx(out=u_codes[:, g, :].bitcast(FP8X4), scales=u_scales[:, g, :], in_=u_grouped[:])
-
-        spread(1, vec_sorted, nw_all)
-        spread(2, vec_rows, b2_all)
 
         hb = [keep.tile([P, HIDDEN], F32, name="hb%d" % m) for m in range(ROW_TILES)]
+        hn = [keep.tile([P, HIDDEN], F32, name="hn%d" % m) for m in range(ROW_TILES)]
         squares = keep.tile([P, ROW_TILES, HIDDEN], BF16)
-        sumsq = [keep.tile([P, CHUNKS1], F32, name="sumsq%d" % m) for m in range(ROW_TILES)]
+        sumsq = [keep.tile([P, GROUPS + 1], F32, name="sumsq%d" % m) for m in range(ROW_TILES)]
+        nc.vector.memset(sumsq[1][:], 0.0)
 
-        def layer1(m, c):
-            cols = slice(c * BANK, (c + 1) * BANK)
+        def pairs_of(natural):
+            return natural.rearrange("q (p w e) -> q w p e", w=PAIRS, e=2)
+
+        def sorted_of(rows, c0, width):
+            g, first = divmod(c0, K_PASS)
+            group = rows[:, g * K_PASS : (g + 1) * K_PASS].rearrange("q (w p e) -> q w p e", w=PAIRS, e=2)
+            return group[:, :, first // PACK : (first + width) // PACK, :]
+
+        def passes1(m, c0, width):
+            cols = slice(c0, c0 + width)
             acc = psum.tile([P, BANK], F32, tag="bank", name="acc1")
             for g in range(PASSES1):
                 nc.tensor.matmul_mx(
-                    out=acc[:],
+                    out=acc[:, 0:width],
                     lhsT=u_codes[:, g, m * P : (m + 1) * P].bitcast(FP8X4),
                     lhsT_scale=u_scales[:, g, m * P : (m + 1) * P],
                     rhs=w1_words[:, g, cols].bitcast(FP8X4),
@@ -153,27 +189,33 @@ def tile_mamba2backbone_pa_kernel(
                     start=(g == 0),
                     stop=(g == PASSES1 - 1),
                 )
+            return acc
+
+        def add_b1(acc, m, c0, width):
+            cols = slice(c0, c0 + width)
             nc.vector.tensor_tensor(
-                out=hb[m][:, cols].rearrange("q (t p) -> q t p", t=PACK),
-                in0=acc[:].rearrange("q (p t) -> q t p", t=PACK),
-                in1=b1_all[:, cols].rearrange("q (t p) -> q t p", t=PACK),
-                op=ALU.add,
+                out=sorted_of(hb[m], c0, width), in0=pairs_of(acc[:, 0:width]), in1=pairs_of(b1_all[:, cols]), op=ALU.add
             )
+
+        def square(m, c0, width, part):
             nc.scalar.activation(
-                out=squares[:, m, cols], in_=hb[m][:, cols], func=ACT.Square, accum_out=sumsq[m][:, c : c + 1]
+                out=sorted_of(squares[:, m, :], c0, width),
+                in_=sorted_of(hb[m], c0, width),
+                func=ACT.Square,
+                accum_out=sumsq[m][:, part : part + 1],
             )
 
-        for step in range(CHUNKS1 + LAG):
-            if step < CHUNKS1:
-                layer1(0, step)
-            if step >= LAG:
-                layer1(1, step - LAG)
+        def gain(engine, m, g):
+            c0 = g * K_PASS
+            engine.tensor_tensor(
+                out=sorted_of(hn[m], c0, K_PASS),
+                in0=sorted_of(hb[m], c0, K_PASS),
+                in1=pairs_of(nw_all[:, c0 : c0 + K_PASS]),
+                op=ALU.mult,
+            )
 
-        g_codes = [keep.tile([P, PASSES2, P], U32, align_bytes=64, name="g_codes%d" % m) for m in range(ROW_TILES)]
-        g_scales = [keep.tile([P, PASSES2, P], U8, align_bytes=64, name="g_scales%d" % m) for m in range(ROW_TILES)]
-
-        def activations(m):
-            parts = stage.tile([P, CHUNKS1], F32, name="parts")
+        def norm(m):
+            parts = stage.tile([P, GROUPS + 1], F32, name="parts")
             mean_eps = stage.tile([P, 1], F32, name="mean_eps")
             rstd = stage.tile([P, 1], F32, name="rstd")
             nc.vector.tensor_scalar(
@@ -181,34 +223,36 @@ def tile_mamba2backbone_pa_kernel(
                 accum_out=mean_eps[:],
             )
             nc.gpsimd.tensor_tensor(out=rstd[:], in0=mean_eps[:], in1=neg_half[:], op=ALU.pow)
-            grouped = []
-            for g in range(PASSES2):
-                cols = slice(g * K_PASS, (g + 1) * K_PASS)
-                hv = stage.tile([P, K_PASS], F32, name="hv")
-                nc.vector.scalar_tensor_tensor(
-                    out=hv[:], in0=hb[m][:, cols], scalar=rstd[:, 0:1], in1=nw_all[:, cols], op0=ALU.mult, op1=ALU.mult
-                )
-                gt = psum.tile([P, PACK, P], F32, tag="bank", name="gt")
-                for t in range(PACK):
-                    nc.tensor.transpose(out=gt[:, t, :], in_=hv[:, t * P : (t + 1) * P], identity=ident_f32[:])
-                g_grouped = stage.tile([P, P * PACK], BF16, align_bytes=64, name="g_grouped", bufs=4)
-                nc.scalar.activation(
-                    out=g_grouped[:].rearrange("p (b t) -> p b t", t=PACK),
-                    in_=gt[:].rearrange("p t b -> p b t"),
-                    func=ACT.Silu,
-                )
-                grouped.append(g_grouped)
-                if g > 0:
-                    quantise(m, g - 1, grouped[g - 1])
-            quantise(m, PASSES2 - 1, grouped[PASSES2 - 1])
+            return rstd
 
-        def quantise(m, g, g_grouped):
+        g_codes = [keep.tile([P, PASSES2, P], U32, align_bytes=64, name="g_codes%d" % m) for m in range(ROW_TILES)]
+        g_scales = [keep.tile([P, PASSES2, P], U8, align_bytes=64, name="g_scales%d" % m) for m in range(ROW_TILES)]
+
+        def silu(m, g, rstd):
+            g_rows = stage.tile([P, K_PASS], BF16, name="g_rows")
+            nc.scalar.activation(
+                out=g_rows[:], in_=hn[m][:, g * K_PASS : (g + 1) * K_PASS], func=ACT.Silu, scale=rstd[:, 0:1]
+            )
+            return g_rows
+
+        def g_turn(g_rows):
+            words = g_rows[:].bitcast(F32)
+            gt = psum.tile([P, PAIRS, P], F32, tag="bank", name="gt")
+            for w in range(PAIRS):
+                nc.tensor.transpose(out=gt[:, w, :], in_=words[:, w * P : (w + 1) * P], identity=ident_f32[:])
+            g_grouped = stage.tile([P, P * PACK], BF16, align_bytes=64, name="g_grouped")
+            nc.vector.tensor_copy(
+                out=g_grouped[:].bitcast(F32).rearrange("p (b w) -> p b w", w=PAIRS), in_=gt[:].rearrange("p w b -> p b w")
+            )
+            return g_grouped
+
+        def g_quantise(m, g, g_grouped):
             nc.vector.quantize_mx(out=g_codes[m][:, g, :].bitcast(FP8X4), scales=g_scales[m][:, g, :], in_=g_grouped[:])
 
-        def pass2(acc, m, g, n):
-            cols = slice(n * BANK, (n + 1) * BANK)
+        def pass2(acc, m, g, c0, width):
+            cols = slice(c0, c0 + width)
             nc.tensor.matmul_mx(
-                out=acc[:],
+                out=acc[:, 0:width],
                 lhsT=g_codes[m][:, g, :].bitcast(FP8X4),
                 lhsT_scale=g_scales[m][:, g, :],
                 rhs=w2_words[:, g, cols].bitcast(FP8X4),
@@ -217,23 +261,114 @@ def tile_mamba2backbone_pa_kernel(
                 stop=(g == PASSES2 - 1),
             )
 
-        def finish(acc, m, n):
-            cols = slice(n * BANK, (n + 1) * BANK)
-            result = stage.tile([P, BANK], F32, name="result", bufs=4)
-            nc.vector.tensor_tensor(out=result[:], in0=acc[:], in1=b2_all[:, cols], op=ALU.add)
-            nc.sync.dma_start(out=out[m * P : (m + 1) * P, cols], in_=result[:])
-
-        activations(0)
-        acc0 = [psum.tile([P, BANK], F32, tag="bank", name="acc2_%d" % n) for n in range(CHUNKS2)]
-        for g in range(PASSES2):
-            if g == PASSES2 // 2:
-                activations(1)
-            for n in range(CHUNKS2):
-                pass2(acc0[n], 0, g, n)
-        for n in range(CHUNKS2):
-            finish(acc0[n], 0, n)
-        for n in range(CHUNKS2):
+        def new_acc():
             acc = psum.tile([P, BANK], F32, tag="bank", name="acc2")
+            return acc
+
+        def finish(acc, m, c0, width):
+            cols = slice(c0, c0 + width)
+            result = stage.tile([P, BANK], F32, name="result", bufs=4)
+            nc.vector.tensor_tensor(out=result[:, 0:width], in0=acc[:, 0:width], in1=b2_all[:, cols], op=ALU.add)
+            nc.sync.dma_start(out=out[m * P : (m + 1) * P, cols], in_=result[:, 0:width])
+
+        def layer2(m, c0, width):
+            acc = new_acc()
             for g in range(PASSES2):
-                pass2(acc, 1, g, n)
-            finish(acc, 1, n)
+                pass2(acc, m, g, c0, width)
+            finish(acc, m, c0, width)
+
+        def layer1(m, c0, width, part):
+            acc = passes1(m, c0, width)
+            add_b1(acc, m, c0, width)
+            square(m, c0, width, part)
+
+        C0, C1, C2, C3 = (c * BANK for c in range(GROUPS))
+        banks = spread(vec_rows[0])
+        spread_copy(nc.scalar.copy, banks, 0, b1_all)
+        spread_copy(nc.vector.tensor_copy, banks, 1, b1_all)
+        layer1(0, C0, BANK, 0)
+        banks = spread(vec_rows[1])
+        spread_copy(nc.scalar.copy, banks, 0, nw_all)
+        spread_copy(nc.vector.tensor_copy, banks, 1, nw_all)
+        layer1(1, C0, BANK, 0)
+        gain(nc.gpsimd, 0, 0)
+        layer1(0, C1, BANK, 1)
+        gain(nc.gpsimd, 1, 0)
+        layer1(0, C2, BANK, 2)
+        gain(nc.vector, 0, 1)
+        layer1(0, C3, HALF, 3)
+        layer1(0, C3 + HALF, HALF, 4)
+        gain(nc.vector, 0, 2)
+        rstd0 = norm(0)
+        gain(nc.vector, 0, 3)
+        acc = passes1(1, C1, BANK)
+        add_b1(acc, 1, C1, BANK)
+        rows0 = [silu(0, g, rstd0) for g in range(2)]
+        square(1, C1, BANK, 1)
+        gain(nc.gpsimd, 1, 1)
+        acc = passes1(1, C2, BANK)
+        add_b1(acc, 1, C2, BANK)
+        rows0.append(silu(0, 2, rstd0))
+        square(1, C2, BANK, 2)
+        acc = passes1(1, C3, BANK)
+        add_b1(acc, 1, C3, BANK)
+        rows0.append(silu(0, 3, rstd0))
+        square(1, C3, BANK, 3)
+        b2_banks = spread(vec_rows[2])
+        accs = [new_acc(), new_acc()]
+
+        def block_a(g):
+            for n in range(2):
+                pass2(accs[n], 0, g, n * BANK, BANK)
+
+        grouped0 = [g_turn(rows0[0])]
+        g_quantise(0, 0, grouped0[0])
+        grouped0.append(g_turn(rows0[1]))
+        g_quantise(0, 1, grouped0[1])
+        block_a(0)
+        grouped0.append(g_turn(rows0[2]))
+        rstd1 = norm(1)
+        g_quantise(0, 2, grouped0[2])
+        block_a(1)
+        grouped0.append(g_turn(rows0[3]))
+        g_quantise(0, 3, grouped0[3])
+        gain(nc.vector, 1, 2)
+        gain(nc.vector, 1, 3)
+        spread_copy(nc.vector.tensor_copy, b2_banks, 0, b2_all)
+        block_a(2)
+        block_a(3)
+        finish(accs[0], 0, 0, BANK)
+        rows1 = [silu(1, g, rstd1) for g in range(GROUPS)]
+        spread_copy(nc.scalar.copy, b2_banks, 1, b2_all)
+        acc2 = new_acc()
+        for g in range(PASSES2):
+            pass2(acc2, 0, g, 2 * BANK, BANK)
+        grouped1 = [g_turn(rows1[0])]
+        g_quantise(1, 0, grouped1[0])
+        grouped1.append(g_turn(rows1[1]))
+        g_quantise(1, 1, grouped1[1])
+        finish(accs[1], 0, BANK, BANK)
+        acc3 = new_acc()
+        for g in range(PASSES2):
+            pass2(acc3, 0, g, 3 * BANK, BANK)
+        grouped1.append(g_turn(rows1[2]))
+        g_quantise(1, 2, grouped1[2])
+        accs1 = [new_acc(), new_acc()]
+
+        def block_b(g):
+            for n in range(2):
+                pass2(accs1[n], 1, g, n * BANK, BANK)
+
+        block_b(0)
+        grouped1.append(g_turn(rows1[3]))
+        g_quantise(1, 3, grouped1[3])
+        finish(acc2, 0, 2 * BANK, BANK)
+        block_b(1)
+        finish(acc3, 0, 3 * BANK, BANK)
+        block_b(2)
+        block_b(3)
+        finish(accs1[0], 1, 0, BANK)
+        finish(accs1[1], 1, BANK, BANK)
+        layer2(1, 2 * BANK, BANK)
+        layer2(1, 3 * BANK, HALF)
+        layer2(1, 3 * BANK + HALF, HALF)

@@ -24,6 +24,7 @@ PASSES1 = K1 // K_PASS
 PASSES2 = HIDDEN // K_PASS
 GROUPS = HIDDEN // K_PASS
 HALF = BANK // 2
+WARM_UPS = 5
 CHUNKS2 = DETER // BANK
 EPS = 1e-4
 PAIRS = 2
@@ -54,6 +55,8 @@ def tile_mamba2backbone_pa_kernel(
         nc.vector.memset(w2_planes[:].bitcast(I32), 0)
         ident_bf = keep.tile([P, P], BF16)
         ident_f32 = keep.tile([P, P], F32)
+        idle_rows = keep.tile([P, BANK], BF16)
+        nc.gpsimd.memset(idle_rows[:].bitcast(I32), 0)
         make_identity(nc, ident_f32[:])
 
         def load_vector(queue, i, vec):
@@ -105,6 +108,24 @@ def tile_mamba2backbone_pa_kernel(
                 in_=w2_dram[:, :, n * BANK * PACK : (n + 1) * BANK * PACK].bitcast(I32),
             )
 
+        def spread(rows, half):
+            bank = psum.tile([P, 2, BANK], BF16, tag="bank", name="spread_bank")
+            for j in range(2):
+                c = 2 * half + j
+                nc.tensor.matmul(
+                    out=bank[:, j, :],
+                    lhsT=ident_bf[:, 32 * c : 32 * c + 1].to_broadcast([P, P]),
+                    rhs=rows[:],
+                    start=True,
+                    stop=True,
+                )
+            return bank
+
+        def spread_copy(copy, bank, half, dest):
+            copy(
+                out=dest[:, 2 * half * BANK : 2 * (half + 1) * BANK], in_=bank[:].rearrange("q j n -> q (j n)")
+            )
+
         u_codes = keep.tile([P, PASSES1, BATCH], U32, align_bytes=64)
         u_scales = keep.tile([P, PASSES1, BATCH], U8, align_bytes=64)
         u_grouped = [keep.tile([P, BATCH * PACK], BF16, align_bytes=64, name="u_grouped%d" % g) for g in range(PASSES1)]
@@ -130,33 +151,16 @@ def tile_mamba2backbone_pa_kernel(
         nc.vector.tensor_scalar(
             out=action_rows[:], in0=action_rows[:], scalar1=-1.0, scalar2=1.0, op0=ALU.max, op1=ALU.min
         )
+        idle = psum.tile([P, BANK], F32, tag="bank", name="idle")
+        for i in range(WARM_UPS):
+            nc.tensor.matmul(out=idle[:], lhsT=idle_rows[:, 0:P], rhs=idle_rows[:], start=True, stop=True)
         u_turn(0)
         u_turn(1)
         u_quantise(0)
         u_turn(2)
+        banks = [spread(vec_rows[0], half) for half in range(2)]
         u_quantise(1)
         u_quantise(2)
-
-        def spread(rows):
-            banks = []
-            for half in range(2):
-                bank = psum.tile([P, 2, BANK], BF16, tag="bank", name="spread_bank")
-                for j in range(2):
-                    c = 2 * half + j
-                    nc.tensor.matmul(
-                        out=bank[:, j, :],
-                        lhsT=ident_bf[:, 32 * c : 32 * c + 1].to_broadcast([P, P]),
-                        rhs=rows[:],
-                        start=True,
-                        stop=True,
-                    )
-                banks.append(bank)
-            return banks
-
-        def spread_copy(copy, banks, half, dest):
-            copy(
-                out=dest[:, 2 * half * BANK : 2 * (half + 1) * BANK], in_=banks[half][:].rearrange("q j n -> q (j n)")
-            )
 
         b1_all = keep.tile([P, HIDDEN], BF16)
         nw_all = keep.tile([P, HIDDEN], BF16)
@@ -235,13 +239,13 @@ def tile_mamba2backbone_pa_kernel(
             )
             return g_rows
 
-        def g_turn(g_rows):
+        def g_turn(g_rows, copy=nc.vector.tensor_copy):
             words = g_rows[:].bitcast(F32)
             gt = psum.tile([P, PAIRS, P], F32, tag="bank", name="gt")
             for w in range(PAIRS):
                 nc.tensor.transpose(out=gt[:, w, :], in_=words[:, w * P : (w + 1) * P], identity=ident_f32[:])
             g_grouped = stage.tile([P, P * PACK], BF16, align_bytes=64, name="g_grouped")
-            nc.vector.tensor_copy(
+            copy(
                 out=g_grouped[:].bitcast(F32).rearrange("p (b w) -> p b w", w=PAIRS), in_=gt[:].rearrange("p w b -> p b w")
             )
             return g_grouped
@@ -267,7 +271,7 @@ def tile_mamba2backbone_pa_kernel(
 
         def finish(acc, m, c0, width):
             cols = slice(c0, c0 + width)
-            result = stage.tile([P, BANK], F32, name="result", bufs=4)
+            result = stage.tile([P, BANK], F32, name="result", bufs=9)
             nc.vector.tensor_tensor(out=result[:, 0:width], in0=acc[:, 0:width], in1=b2_all[:, cols], op=ALU.add)
             nc.sync.dma_start(out=out[m * P : (m + 1) * P, cols], in_=result[:, 0:width])
 
@@ -283,13 +287,12 @@ def tile_mamba2backbone_pa_kernel(
             square(m, c0, width, part)
 
         C0, C1, C2, C3 = (c * BANK for c in range(GROUPS))
-        banks = spread(vec_rows[0])
-        spread_copy(nc.scalar.copy, banks, 0, b1_all)
-        spread_copy(nc.vector.tensor_copy, banks, 1, b1_all)
+        spread_copy(nc.scalar.copy, banks[0], 0, b1_all)
+        spread_copy(nc.vector.tensor_copy, banks[1], 1, b1_all)
         layer1(0, C0, BANK, 0)
-        banks = spread(vec_rows[1])
-        spread_copy(nc.scalar.copy, banks, 0, nw_all)
-        spread_copy(nc.vector.tensor_copy, banks, 1, nw_all)
+        banks = [spread(vec_rows[1], half) for half in range(2)]
+        spread_copy(nc.scalar.copy, banks[0], 0, nw_all)
+        spread_copy(nc.vector.tensor_copy, banks[1], 1, nw_all)
         layer1(1, C0, BANK, 0)
         gain(nc.gpsimd, 0, 0)
         layer1(0, C1, BANK, 1)
@@ -314,7 +317,7 @@ def tile_mamba2backbone_pa_kernel(
         add_b1(acc, 1, C3, BANK)
         rows0.append(silu(0, 3, rstd0))
         square(1, C3, BANK, 3)
-        b2_banks = spread(vec_rows[2])
+        b2_banks = [spread(vec_rows[2], half) for half in range(2)]
         accs = [new_acc(), new_acc()]
 
         def block_a(g):
@@ -334,12 +337,12 @@ def tile_mamba2backbone_pa_kernel(
         g_quantise(0, 3, grouped0[3])
         gain(nc.vector, 1, 2)
         gain(nc.vector, 1, 3)
-        spread_copy(nc.vector.tensor_copy, b2_banks, 0, b2_all)
+        spread_copy(nc.vector.tensor_copy, b2_banks[0], 0, b2_all)
         block_a(2)
         block_a(3)
         finish(accs[0], 0, 0, BANK)
         rows1 = [silu(1, g, rstd1) for g in range(GROUPS)]
-        spread_copy(nc.scalar.copy, b2_banks, 1, b2_all)
+        spread_copy(nc.scalar.copy, b2_banks[1], 1, b2_all)
         acc2 = new_acc()
         for g in range(PASSES2):
             pass2(acc2, 0, g, 2 * BANK, BANK)

@@ -151,6 +151,17 @@ def tile_mamba2backbone_pa_kernel(
         nc.vector.tensor_scalar(
             out=action_rows[:], in0=action_rows[:], scalar1=-1.0, scalar2=1.0, op0=ALU.max, op1=ALU.min
         )
+        def pairs_of(natural):
+            return natural.rearrange("q (p w e) -> q w p e", w=PAIRS, e=2)
+
+        sorted_rows = [keep.tile([P, BANK], BF16, name="sorted_rows%d" % i) for i in range(2)]
+
+        def sort_vector(copy, i):
+            copy(
+                out=sorted_rows[i][:].rearrange("q (w p e) -> q w p e", w=PAIRS, e=2), in_=pairs_of(vec_rows[i][:])
+            )
+
+        sort_vector(nc.scalar.copy, 0)
         idle = psum.tile([P, BANK], F32, tag="bank", name="idle")
         for i in range(WARM_UPS):
             nc.tensor.matmul(out=idle[:], lhsT=idle_rows[:, 0:P], rhs=idle_rows[:], start=True, stop=True)
@@ -158,9 +169,10 @@ def tile_mamba2backbone_pa_kernel(
         u_turn(1)
         u_quantise(0)
         u_turn(2)
-        banks = [spread(vec_rows[0], half) for half in range(2)]
+        banks = [spread(sorted_rows[0], half) for half in range(2)]
         u_quantise(1)
         u_quantise(2)
+        sort_vector(nc.vector.tensor_copy, 1)
 
         b1_all = keep.tile([P, HIDDEN], BF16)
         nw_all = keep.tile([P, HIDDEN], BF16)
@@ -171,9 +183,6 @@ def tile_mamba2backbone_pa_kernel(
         squares = keep.tile([P, ROW_TILES, HIDDEN], BF16)
         sumsq = [keep.tile([P, GROUPS + 1], F32, name="sumsq%d" % m) for m in range(ROW_TILES)]
         nc.vector.memset(sumsq[1][:], 0.0)
-
-        def pairs_of(natural):
-            return natural.rearrange("q (p w e) -> q w p e", w=PAIRS, e=2)
 
         def sorted_of(rows, c0, width):
             g, first = divmod(c0, K_PASS)
@@ -198,7 +207,7 @@ def tile_mamba2backbone_pa_kernel(
         def add_b1(acc, m, c0, width):
             cols = slice(c0, c0 + width)
             nc.vector.tensor_tensor(
-                out=sorted_of(hb[m], c0, width), in0=pairs_of(acc[:, 0:width]), in1=pairs_of(b1_all[:, cols]), op=ALU.add
+                out=sorted_of(hb[m], c0, width), in0=pairs_of(acc[:, 0:width]), in1=sorted_of(b1_all, c0, width), op=ALU.add
             )
 
         def square(m, c0, width, part):
@@ -212,9 +221,9 @@ def tile_mamba2backbone_pa_kernel(
         def gain(engine, m, g):
             c0 = g * K_PASS
             engine.tensor_tensor(
-                out=sorted_of(hn[m], c0, K_PASS),
-                in0=sorted_of(hb[m], c0, K_PASS),
-                in1=pairs_of(nw_all[:, c0 : c0 + K_PASS]),
+                out=hn[m][:, c0 : c0 + K_PASS],
+                in0=hb[m][:, c0 : c0 + K_PASS],
+                in1=nw_all[:, c0 : c0 + K_PASS],
                 op=ALU.mult,
             )
 
@@ -290,7 +299,7 @@ def tile_mamba2backbone_pa_kernel(
         spread_copy(nc.scalar.copy, banks[0], 0, b1_all)
         spread_copy(nc.vector.tensor_copy, banks[1], 1, b1_all)
         layer1(0, C0, BANK, 0)
-        banks = [spread(vec_rows[1], half) for half in range(2)]
+        banks = [spread(sorted_rows[1], half) for half in range(2)]
         spread_copy(nc.scalar.copy, banks[0], 0, nw_all)
         spread_copy(nc.vector.tensor_copy, banks[1], 1, nw_all)
         layer1(1, C0, BANK, 0)

@@ -102,11 +102,17 @@ def tile_mamba2backbone_pa_kernel(
             )
         w2_words = keep.tile([P, PASSES2, DETER], U32, align_bytes=64)
         w2_dram = tok_w2_words.rearrange("g p n t -> p g (n t)")
-        for n in range(CHUNKS2):
+
+        def load_w2(g0, g1, c0, width):
             nc.sync.dma_start(
-                out=w2_words[:, :, n * BANK : (n + 1) * BANK].bitcast(I32),
-                in_=w2_dram[:, :, n * BANK * PACK : (n + 1) * BANK * PACK].bitcast(I32),
+                out=w2_words[:, g0:g1, c0 : c0 + width].bitcast(I32),
+                in_=w2_dram[:, g0:g1, c0 * PACK : (c0 + width) * PACK].bitcast(I32),
             )
+
+        for g in range(PASSES2):
+            load_w2(g, g + 1, 0, 2 * BANK)
+        for n in range(2, CHUNKS2):
+            load_w2(0, PASSES2, n * BANK, BANK)
 
         def spread(rows, half):
             bank = psum.tile([P, 2, BANK], BF16, tag="bank", name="spread_bank")
@@ -307,80 +313,67 @@ def tile_mamba2backbone_pa_kernel(
         layer1(0, C1, BANK, 1)
         gain(nc.gpsimd, 1, 0)
         layer1(0, C2, BANK, 2)
-        gain(nc.vector, 0, 1)
-        layer1(0, C3, HALF, 3)
-        layer1(0, C3 + HALF, HALF, 4)
-        gain(nc.vector, 0, 2)
-        rstd0 = norm(0)
-        gain(nc.vector, 0, 3)
         acc = passes1(1, C1, BANK)
         add_b1(acc, 1, C1, BANK)
-        rows0 = [silu(0, g, rstd0) for g in range(2)]
-        square(1, C1, BANK, 1)
         gain(nc.gpsimd, 1, 1)
-        acc = passes1(1, C2, BANK)
-        add_b1(acc, 1, C2, BANK)
-        rows0.append(silu(0, 2, rstd0))
+        layer1(0, C3, HALF, 3)
+        layer1(0, C3 + HALF, HALF, 4)
+        square(1, C1, BANK, 1)
+        gain(nc.vector, 0, 1)
+        rstd0 = norm(0)
+        for c0, part in ((C2, 2), (C3, 3)):
+            acc = passes1(1, c0, BANK)
+            add_b1(acc, 1, c0, BANK)
+        rows0 = [silu(0, g, rstd0) for g in range(2)]
         square(1, C2, BANK, 2)
-        acc = passes1(1, C3, BANK)
-        add_b1(acc, 1, C3, BANK)
-        rows0.append(silu(0, 3, rstd0))
         square(1, C3, BANK, 3)
-        b2_banks = [spread(vec_rows[2], half) for half in range(2)]
+        gain(nc.vector, 0, 2)
+        gain(nc.vector, 0, 3)
+        rows0 += [silu(0, g, rstd0) for g in range(2, GROUPS)]
         accs = [new_acc(), new_acc()]
+        s_copy = nc.scalar.copy
 
         def block_a(g):
             for n in range(2):
                 pass2(accs[n], 0, g, n * BANK, BANK)
 
+        b2_banks = [spread(vec_rows[2], 0)]
         grouped0 = [g_turn(rows0[0])]
         g_quantise(0, 0, grouped0[0])
+        b2_banks.append(spread(vec_rows[2], 1))
         grouped0.append(g_turn(rows0[1]))
+        rstd1 = norm(1)
         g_quantise(0, 1, grouped0[1])
         block_a(0)
         grouped0.append(g_turn(rows0[2]))
-        rstd1 = norm(1)
         g_quantise(0, 2, grouped0[2])
         block_a(1)
         grouped0.append(g_turn(rows0[3]))
-        g_quantise(0, 3, grouped0[3])
         gain(nc.vector, 1, 2)
+        g_quantise(0, 3, grouped0[3])
         gain(nc.vector, 1, 3)
-        spread_copy(nc.vector.tensor_copy, b2_banks[0], 0, b2_all)
         block_a(2)
         block_a(3)
-        finish(accs[0], 0, 0, BANK)
+        spread_copy(s_copy, b2_banks[0], 0, b2_all)
         rows1 = [silu(1, g, rstd1) for g in range(GROUPS)]
-        spread_copy(nc.scalar.copy, b2_banks[1], 1, b2_all)
-        acc2 = new_acc()
-        for g in range(PASSES2):
-            pass2(acc2, 0, g, 2 * BANK, BANK)
-        grouped1 = [g_turn(rows1[0])]
-        g_quantise(1, 0, grouped1[0])
-        grouped1.append(g_turn(rows1[1]))
-        g_quantise(1, 1, grouped1[1])
+        finish(accs[0], 0, 0, BANK)
         finish(accs[1], 0, BANK, BANK)
-        acc3 = new_acc()
-        for g in range(PASSES2):
-            pass2(acc3, 0, g, 3 * BANK, BANK)
-        grouped1.append(g_turn(rows1[2]))
-        g_quantise(1, 2, grouped1[2])
-        accs1 = [new_acc(), new_acc()]
-
-        def block_b(g):
-            for n in range(2):
-                pass2(accs1[n], 1, g, n * BANK, BANK)
-
-        block_b(0)
-        grouped1.append(g_turn(rows1[3]))
-        g_quantise(1, 3, grouped1[3])
+        grouped1 = [g_turn(rows1[g], s_copy) for g in range(2)]
+        acc2 = new_acc()
+        for g in range(2):
+            pass2(acc2, 0, g, 2 * BANK, BANK)
+        for g in range(2):
+            g_quantise(1, g, grouped1[g])
+        grouped1 += [g_turn(rows1[g], s_copy) for g in range(2, GROUPS)]
+        spread_copy(s_copy, b2_banks[1], 1, b2_all)
+        for g in range(2, PASSES2):
+            pass2(acc2, 0, g, 2 * BANK, BANK)
+        for g in range(2, GROUPS):
+            g_quantise(1, g, grouped1[g])
         finish(acc2, 0, 2 * BANK, BANK)
-        block_b(1)
-        finish(acc3, 0, 3 * BANK, BANK)
-        block_b(2)
-        block_b(3)
-        finish(accs1[0], 1, 0, BANK)
-        finish(accs1[1], 1, BANK, BANK)
+        layer2(1, 0, BANK)
+        layer2(1, BANK, BANK)
+        layer2(0, 3 * BANK, BANK)
         layer2(1, 2 * BANK, BANK)
         layer2(1, 3 * BANK, HALF)
         layer2(1, 3 * BANK + HALF, HALF)

@@ -247,11 +247,16 @@ def tile_mamba2backbone_pa_kernel(
         g_codes = [keep.tile([P, PASSES2, P], U32, align_bytes=64, name="g_codes%d" % m) for m in range(ROW_TILES)]
         g_scales = [keep.tile([P, PASSES2, P], U8, align_bytes=64, name="g_scales%d" % m) for m in range(ROW_TILES)]
 
-        def silu(m, g, rstd):
+        def silu(m, g, rstd, parts=1):
             g_rows = stage.tile([P, K_PASS], BF16, name="g_rows")
-            nc.scalar.activation(
-                out=g_rows[:], in_=hn[m][:, g * K_PASS : (g + 1) * K_PASS], func=ACT.Silu, scale=rstd[:, 0:1]
-            )
+            width = K_PASS // parts
+            for c in range(0, K_PASS, width):
+                nc.scalar.activation(
+                    out=g_rows[:, c : c + width],
+                    in_=hn[m][:, g * K_PASS + c : g * K_PASS + c + width],
+                    func=ACT.Silu,
+                    scale=rstd[:, 0:1],
+                )
             return g_rows
 
         def g_turn(g_rows, copy=nc.vector.tensor_copy):
@@ -303,33 +308,34 @@ def tile_mamba2backbone_pa_kernel(
 
         C0, C1, C2, C3 = (c * BANK for c in range(GROUPS))
         spread_copy(nc.scalar.copy, banks[0], 0, b1_all)
-        spread_copy(nc.vector.tensor_copy, banks[1], 1, b1_all)
+        spread_copy(nc.scalar.copy, banks[1], 1, b1_all)
         layer1(0, C0, BANK, 0)
         banks = [spread(sorted_rows[1], half) for half in range(2)]
         spread_copy(nc.scalar.copy, banks[0], 0, nw_all)
-        spread_copy(nc.vector.tensor_copy, banks[1], 1, nw_all)
+        spread_copy(nc.scalar.copy, banks[1], 1, nw_all)
         layer1(1, C0, BANK, 0)
         gain(nc.gpsimd, 0, 0)
         layer1(0, C1, BANK, 1)
+        gain(nc.gpsimd, 0, 1)
         gain(nc.gpsimd, 1, 0)
         layer1(0, C2, BANK, 2)
         acc = passes1(1, C1, BANK)
         add_b1(acc, 1, C1, BANK)
-        gain(nc.gpsimd, 1, 1)
         layer1(0, C3, HALF, 3)
         layer1(0, C3 + HALF, HALF, 4)
         square(1, C1, BANK, 1)
-        gain(nc.vector, 0, 1)
+        gain(nc.vector, 0, 2)
         rstd0 = norm(0)
         for c0, part in ((C2, 2), (C3, 3)):
             acc = passes1(1, c0, BANK)
             add_b1(acc, 1, c0, BANK)
-        rows0 = [silu(0, g, rstd0) for g in range(2)]
+        rows0 = [silu(0, 0, rstd0, parts=2), silu(0, 1, rstd0)]
         square(1, C2, BANK, 2)
+        rows0.append(silu(0, 2, rstd0))
         square(1, C3, BANK, 3)
-        gain(nc.vector, 0, 2)
-        gain(nc.vector, 0, 3)
-        rows0 += [silu(0, g, rstd0) for g in range(2, GROUPS)]
+        gain(nc.gpsimd, 0, 3)
+        gain(nc.gpsimd, 1, 1)
+        rows0.append(silu(0, 3, rstd0))
         accs = [new_acc(), new_acc()]
         s_copy = nc.scalar.copy
 
@@ -342,14 +348,14 @@ def tile_mamba2backbone_pa_kernel(
         g_quantise(0, 0, grouped0[0])
         b2_banks.append(spread(vec_rows[2], 1))
         grouped0.append(g_turn(rows0[1]))
-        rstd1 = norm(1)
         g_quantise(0, 1, grouped0[1])
+        rstd1 = norm(1)
         block_a(0)
         grouped0.append(g_turn(rows0[2]))
+        gain(nc.vector, 1, 2)
         g_quantise(0, 2, grouped0[2])
         block_a(1)
         grouped0.append(g_turn(rows0[3]))
-        gain(nc.vector, 1, 2)
         g_quantise(0, 3, grouped0[3])
         gain(nc.vector, 1, 3)
         block_a(2)

@@ -75,10 +75,10 @@ def tile_mamba2backbone_pa_kernel(
         w1_words = keep.tile([P, PASSES1, HIDDEN], U32, align_bytes=64)
         w1_dram = tok_w1_words.rearrange("g p n t -> p g (n t)")
 
-        def load_w1(c0, width):
+        def load_w1(c0, width, g0=0, g1=PASSES1):
             nc.sync.dma_start(
-                out=w1_words[:, :, c0 : c0 + width].bitcast(I32),
-                in_=w1_dram[:, :, c0 * PACK : (c0 + width) * PACK].bitcast(I32),
+                out=w1_words[:, g0:g1, c0 : c0 + width].bitcast(I32),
+                in_=w1_dram[:, g0:g1, c0 * PACK : (c0 + width) * PACK].bitcast(I32),
             )
 
         def load_w1_scales(q):
@@ -93,8 +93,9 @@ def tile_mamba2backbone_pa_kernel(
             load_w1_scales(q)
         load_w1(BANK, BANK)
         load_w1(2 * BANK, BANK)
-        load_w1(3 * BANK, HALF)
-        load_w1(3 * BANK + HALF, HALF)
+        load_w1(3 * BANK, BANK, 0, PASSES1 - 1)
+        load_w1(3 * BANK, HALF, PASSES1 - 1, PASSES1)
+        load_w1(3 * BANK + HALF, HALF, PASSES1 - 1, PASSES1)
         for q in range(4):
             nc.sync.dma_start(
                 out=w2_planes[32 * q : 32 * q + 4 * PASSES2, :].bitcast(I32),
@@ -110,9 +111,7 @@ def tile_mamba2backbone_pa_kernel(
             )
 
         for g in range(PASSES2):
-            load_w2(g, g + 1, 0, 2 * BANK)
-        for n in range(2, CHUNKS2):
-            load_w2(0, PASSES2, n * BANK, BANK)
+            load_w2(g, g + 1, 0, DETER)
 
         def spread(rows, half):
             bank = psum.tile([P, 2, BANK], BF16, tag="bank", name="spread_bank")
@@ -168,9 +167,12 @@ def tile_mamba2backbone_pa_kernel(
             )
 
         sort_vector(nc.scalar.copy, 0)
-        idle = psum.tile([P, BANK], F32, tag="bank", name="idle")
-        for i in range(WARM_UPS):
-            nc.tensor.matmul(out=idle[:], lhsT=idle_rows[:, 0:P], rhs=idle_rows[:], start=True, stop=True)
+        def idle_products(count):
+            idle = psum.tile([P, BANK], F32, tag="bank", name="idle")
+            for i in range(count):
+                nc.tensor.matmul(out=idle[:], lhsT=idle_rows[:, 0:P], rhs=idle_rows[:], start=True, stop=True)
+
+        idle_products(WARM_UPS)
         u_turn(0)
         u_turn(1)
         u_quantise(0)
@@ -336,11 +338,11 @@ def tile_mamba2backbone_pa_kernel(
         gain(nc.gpsimd, 0, 3)
         gain(nc.gpsimd, 1, 1)
         rows0.append(silu(0, 3, rstd0))
-        accs = [new_acc(), new_acc()]
+        accs = [new_acc() for n in range(CHUNKS2)]
         s_copy = nc.scalar.copy
 
         def block_a(g):
-            for n in range(2):
+            for n in range(CHUNKS2):
                 pass2(accs[n], 0, g, n * BANK, BANK)
 
         b2_banks = [spread(vec_rows[2], 0)]
@@ -350,36 +352,28 @@ def tile_mamba2backbone_pa_kernel(
         grouped0.append(g_turn(rows0[1]))
         g_quantise(0, 1, grouped0[1])
         rstd1 = norm(1)
+        for half in range(2):
+            spread_copy(s_copy, b2_banks[half], half, b2_all)
+        gain(nc.vector, 1, 2)
         block_a(0)
         grouped0.append(g_turn(rows0[2]))
-        gain(nc.vector, 1, 2)
+        gain(nc.vector, 1, 3)
         g_quantise(0, 2, grouped0[2])
         block_a(1)
         grouped0.append(g_turn(rows0[3]))
         g_quantise(0, 3, grouped0[3])
-        gain(nc.vector, 1, 3)
         block_a(2)
-        block_a(3)
-        spread_copy(s_copy, b2_banks[0], 0, b2_all)
         rows1 = [silu(1, g, rstd1) for g in range(GROUPS)]
-        finish(accs[0], 0, 0, BANK)
-        finish(accs[1], 0, BANK, BANK)
-        grouped1 = [g_turn(rows1[g], s_copy) for g in range(2)]
-        acc2 = new_acc()
-        for g in range(2):
-            pass2(acc2, 0, g, 2 * BANK, BANK)
+        grouped1 = [g_turn(rows1[g], s_copy) for g in range(GROUPS)]
+        block_a(3)
         for g in range(2):
             g_quantise(1, g, grouped1[g])
-        grouped1 += [g_turn(rows1[g], s_copy) for g in range(2, GROUPS)]
-        spread_copy(s_copy, b2_banks[1], 1, b2_all)
-        for g in range(2, PASSES2):
-            pass2(acc2, 0, g, 2 * BANK, BANK)
+        finish(accs[0], 0, 0, BANK)
         for g in range(2, GROUPS):
             g_quantise(1, g, grouped1[g])
-        finish(acc2, 0, 2 * BANK, BANK)
-        layer2(1, 0, BANK)
-        layer2(1, BANK, BANK)
-        layer2(0, 3 * BANK, BANK)
-        layer2(1, 2 * BANK, BANK)
+        for n in range(1, CHUNKS2):
+            finish(accs[n], 0, n * BANK, BANK)
+        for n in range(3):
+            layer2(1, n * BANK, BANK)
         layer2(1, 3 * BANK, HALF)
         layer2(1, 3 * BANK + HALF, HALF)

from contextlib import ExitStack

import concourse.mybir as mybir
from concourse.masks import make_identity

F32 = mybir.dt.float32
BF16 = mybir.dt.bfloat16
I32 = mybir.dt.int32
U32 = mybir.dt.uint32
U8 = mybir.dt.uint8
FP8X4 = mybir.dt.float8_e4m3fn_x4
ALU = mybir.AluOpType
ACT = mybir.ActivationFunctionType

P = 128
PACK = 4
K_PASS = P * PACK
BANK = 512

BATCH, STOCH, ACTION, HIDDEN, DETER = 256, 1024, 512, 2048, 2048
K1 = STOCH + ACTION
ROW_TILES = BATCH // P
PASSES1 = K1 // K_PASS
PASSES2 = HIDDEN // K_PASS
GROUPS = HIDDEN // K_PASS
HALF = BANK // 2
WARM_UPS = 5
CHUNKS2 = DETER // BANK
EPS = 1e-4
PAIRS = 2

FLOPS = 2 * BATCH * (K1 * HIDDEN + HIDDEN * DETER)


def tile_mamba2backbone_pa_kernel(
    tc, stoch, action, tok_w1_words, tok_w1_scales, tok_b1, tok_nw, tok_w2_words, tok_w2_scales, tok_b2, out
):
    nc = tc.nc
    with ExitStack() as ctx:
        keep = ctx.enter_context(tc.tile_pool(name="keep", bufs=1))
        stage = ctx.enter_context(tc.tile_pool(name="stage", bufs=4))
        psum = ctx.enter_context(tc.psum_pool(name="psum", bufs=8))

        ctx.enter_context(tc.manual_schedule())
        w1_planes = keep.tile([P, HIDDEN], U8, align_bytes=64)
        w2_planes = keep.tile([P, DETER], U8, align_bytes=64)
        neg_half = keep.tile([P, 1], F32)
        warm = keep.tile([P, 1], F32)
        vec_rows = [keep.tile([P, BANK], BF16, name="vec_rows%d" % i) for i in range(3)]
        nc.vector.memset(w1_planes[:].bitcast(I32), 0)
        nc.vector.memset(vec_rows[0][:].bitcast(I32), 0)
        nc.vector.memset(neg_half[:], -0.5)
        nc.vector.memset(vec_rows[1][:].bitcast(I32), 0)
        nc.vector.memset(vec_rows[2][:].bitcast(I32), 0)
        nc.vector.memset(w2_planes[:].bitcast(I32), 0)
        ident_bf = keep.tile([P, P], BF16)
        ident_f32 = keep.tile([P, P], F32)
        idle_rows = keep.tile([P, BANK], BF16)
        nc.gpsimd.memset(idle_rows[:].bitcast(I32), 0)
        make_identity(nc, ident_f32[:])

        def load_vector(queue, i, vec):
            queue.dma_start(out=vec_rows[i][0:P:32, :], in_=vec.rearrange("(c n) -> c n", n=BANK))

        load_vector(nc.scalar, 0, tok_b1)
        load_vector(nc.gpsimd, 1, tok_nw)
        make_identity(nc, ident_bf[:])
        load_vector(nc.gpsimd, 2, tok_b2)
        nc.scalar.activation(out=warm[:], in_=neg_half[:], func=ACT.Silu)

        stoch_rows = keep.tile([P, ROW_TILES, STOCH], BF16)
        action_rows = keep.tile([P, ROW_TILES, ACTION], BF16)
        nc.sync.dma_start(out=stoch_rows[:], in_=stoch.rearrange("(m p) k -> p m k", p=P))
        nc.sync.dma_start(out=action_rows[:], in_=action.rearrange("(m p) k -> p m k", p=P))
        w1_words = keep.tile([P, PASSES1, HIDDEN], U32, align_bytes=64)
        w1_dram = tok_w1_words.rearrange("g p n t -> p g (n t)")

        def load_w1(c0, width, g0=0, g1=PASSES1):
            nc.sync.dma_start(
                out=w1_words[:, g0:g1, c0 : c0 + width].bitcast(I32),
                in_=w1_dram[:, g0:g1, c0 * PACK : (c0 + width) * PACK].bitcast(I32),
            )

        def load_w1_scales(q):
            nc.sync.dma_start(
                out=w1_planes[32 * q : 32 * q + 4 * PASSES1, :].bitcast(I32),
                in_=tok_w1_scales[:, 4 * q : 4 * q + 4, :].bitcast(I32),
            )

        load_w1_scales(0)
        load_w1(0, BANK)
        for q in range(1, 4):
            load_w1_scales(q)
        load_w1(BANK, BANK)
        load_w1(2 * BANK, BANK)
        load_w1(3 * BANK, BANK, 0, PASSES1 - 1)
        load_w1(3 * BANK, HALF, PASSES1 - 1, PASSES1)
        load_w1(3 * BANK + HALF, HALF, PASSES1 - 1, PASSES1)
        for q in range(4):
            nc.sync.dma_start(
                out=w2_planes[32 * q : 32 * q + 4 * PASSES2, :].bitcast(I32),
                in_=tok_w2_scales[:, 4 * q : 4 * q + 4, :].bitcast(I32),
            )
        w2_words = keep.tile([P, PASSES2, DETER], U32, align_bytes=64)
        w2_dram = tok_w2_words.rearrange("g p n t -> p g (n t)")

        def load_w2(g0, g1, c0, width):
            nc.sync.dma_start(
                out=w2_words[:, g0:g1, c0 : c0 + width].bitcast(I32),
                in_=w2_dram[:, g0:g1, c0 * PACK : (c0 + width) * PACK].bitcast(I32),
            )

        for g in range(PASSES2):
            load_w2(g, g + 1, 0, DETER)

        def spread(rows, half):
            bank = psum.tile([P, 2, BANK], BF16, tag="bank", name="spread_bank")
            for j in range(2):
                c = 2 * half + j
                nc.tensor.matmul(
                    out=bank[:, j, :],
                    lhsT=ident_bf[:, 32 * c : 32 * c + 1].to_broadcast([P, P]),
                    rhs=rows[:],
                    start=True,
                    stop=True,
                )
            return bank

        def spread_copy(copy, bank, half, dest):
            copy(
                out=dest[:, 2 * half * BANK : 2 * (half + 1) * BANK], in_=bank[:].rearrange("q j n -> q (j n)")
            )

        u_codes = keep.tile([P, PASSES1, BATCH], U32, align_bytes=64)
        u_scales = keep.tile([P, PASSES1, BATCH], U8, align_bytes=64)
        u_grouped = [keep.tile([P, BATCH * PACK], BF16, align_bytes=64, name="u_grouped%d" % g) for g in range(PASSES1)]

        def u_turn(g):
            rows, k0 = (stoch_rows, g * K_PASS) if g * K_PASS < STOCH else (action_rows, g * K_PASS - STOCH)
            ut = psum.tile([P, ROW_TILES, PAIRS, P], F32, tag="bank", name="ut")
            for m in range(ROW_TILES):
                words = rows[:, m, k0 : k0 + K_PASS].bitcast(F32)
                for w in range(PAIRS):
                    nc.tensor.transpose(out=ut[:, m, w, :], in_=words[:, w::2], identity=ident_f32[:])
            copy = nc.scalar.copy if g == 1 else nc.vector.tensor_copy
            copy(
                out=u_grouped[g][:].bitcast(F32).rearrange("p (m b w) -> p m b w", m=ROW_TILES, w=PAIRS),
                in_=ut[:].rearrange("p m w b -> p m b w"),
            )

        def u_quantise(g):
            nc.vector.quantize_mx(
                out=u_codes[:, g, :].bitcast(FP8X4), scales=u_scales[:, g, :], in_=u_grouped[g][:]
            )

        nc.vector.tensor_scalar(
            out=action_rows[:], in0=action_rows[:], scalar1=-1.0, scalar2=1.0, op0=ALU.max, op1=ALU.min
        )
        def pairs_of(natural):
            return natural.rearrange("q (p w e) -> q w p e", w=PAIRS, e=2)

        sorted_rows = [keep.tile([P, BANK], BF16, name="sorted_rows%d" % i) for i in range(2)]

        def sort_vector(copy, i):
            copy(
                out=sorted_rows[i][:].rearrange("q (w p e) -> q w p e", w=PAIRS, e=2), in_=pairs_of(vec_rows[i][:])
            )

        sort_vector(nc.scalar.copy, 0)
        def idle_products(count):
            idle = psum.tile([P, BANK], F32, tag="bank", name="idle")
            for i in range(count):
                nc.tensor.matmul(out=idle[:], lhsT=idle_rows[:, 0:P], rhs=idle_rows[:], start=True, stop=True)

        idle_products(WARM_UPS)
        u_turn(0)
        u_turn(1)
        u_quantise(0)
        u_turn(2)
        banks = [spread(sorted_rows[0], half) for half in range(2)]
        u_quantise(1)
        u_quantise(2)
        sort_vector(nc.vector.tensor_copy, 1)

        b1_all = keep.tile([P, HIDDEN], BF16)
        nw_all = keep.tile([P, HIDDEN], BF16)
        b2_all = keep.tile([P, DETER], BF16)

        hb = [keep.tile([P, HIDDEN], F32, name="hb%d" % m) for m in range(ROW_TILES)]
        hn = [keep.tile([P, HIDDEN], F32, name="hn%d" % m) for m in range(ROW_TILES)]
        squares = keep.tile([P, ROW_TILES, HIDDEN], BF16)
        sumsq = [keep.tile([P, GROUPS + 1], F32, name="sumsq%d" % m) for m in range(ROW_TILES)]
        nc.vector.memset(sumsq[1][:], 0.0)

        def sorted_of(rows, c0, width):
            g, first = divmod(c0, K_PASS)
            group = rows[:, g * K_PASS : (g + 1) * K_PASS].rearrange("q (w p e) -> q w p e", w=PAIRS, e=2)
            return group[:, :, first // PACK : (first + width) // PACK, :]

        def passes1(m, c0, width):
            cols = slice(c0, c0 + width)
            acc = psum.tile([P, BANK], F32, tag="bank", name="acc1")
            for g in range(PASSES1):
                nc.tensor.matmul_mx(
                    out=acc[:, 0:width],
                    lhsT=u_codes[:, g, m * P : (m + 1) * P].bitcast(FP8X4),
                    lhsT_scale=u_scales[:, g, m * P : (m + 1) * P],
                    rhs=w1_words[:, g, cols].bitcast(FP8X4),
                    rhs_scale=w1_planes[4 * g : P, cols],
                    start=(g == 0),
                    stop=(g == PASSES1 - 1),
                )
            return acc

        def add_b1(acc, m, c0, width):
            cols = slice(c0, c0 + width)
            nc.vector.tensor_tensor(
                out=sorted_of(hb[m], c0, width), in0=pairs_of(acc[:, 0:width]), in1=sorted_of(b1_all, c0, width), op=ALU.add
            )

        def square(m, c0, width, part):
            nc.scalar.activation(
                out=sorted_of(squares[:, m, :], c0, width),
                in_=sorted_of(hb[m], c0, width),
                func=ACT.Square,
                accum_out=sumsq[m][:, part : part + 1],
            )

        def gain(engine, m, g):
            c0 = g * K_PASS
            engine.tensor_tensor(
                out=hn[m][:, c0 : c0 + K_PASS],
                in0=hb[m][:, c0 : c0 + K_PASS],
                in1=nw_all[:, c0 : c0 + K_PASS],
                op=ALU.mult,
            )

        def norm(m):
            parts = stage.tile([P, GROUPS + 1], F32, name="parts")
            mean_eps = stage.tile([P, 1], F32, name="mean_eps")
            rstd = stage.tile([P, 1], F32, name="rstd")
            nc.vector.tensor_scalar(
                out=parts[:], in0=sumsq[m][:], scalar1=1.0 / HIDDEN, scalar2=EPS, op0=ALU.mult, op1=ALU.add,
                accum_out=mean_eps[:],
            )
            nc.gpsimd.tensor_tensor(out=rstd[:], in0=mean_eps[:], in1=neg_half[:], op=ALU.pow)
            return rstd

        g_codes = [keep.tile([P, PASSES2, P], U32, align_bytes=64, name="g_codes%d" % m) for m in range(ROW_TILES)]
        g_scales = [keep.tile([P, PASSES2, P], U8, align_bytes=64, name="g_scales%d" % m) for m in range(ROW_TILES)]

        def silu(m, g, rstd, parts=1):
            g_rows = stage.tile([P, K_PASS], BF16, name="g_rows")
            width = K_PASS // parts
            for c in range(0, K_PASS, width):
                nc.scalar.activation(
                    out=g_rows[:, c : c + width],
                    in_=hn[m][:, g * K_PASS + c : g * K_PASS + c + width],
                    func=ACT.Silu,
                    scale=rstd[:, 0:1],
                )
            return g_rows

        def g_turn(g_rows, copy=nc.vector.tensor_copy):
            words = g_rows[:].bitcast(F32)
            gt = psum.tile([P, PAIRS, P], F32, tag="bank", name="gt")
            for w in range(PAIRS):
                nc.tensor.transpose(out=gt[:, w, :], in_=words[:, w * P : (w + 1) * P], identity=ident_f32[:])
            g_grouped = stage.tile([P, P * PACK], BF16, align_bytes=64, name="g_grouped")
            copy(
                out=g_grouped[:].bitcast(F32).rearrange("p (b w) -> p b w", w=PAIRS), in_=gt[:].rearrange("p w b -> p b w")
            )
            return g_grouped

        def g_quantise(m, g, g_grouped):
            nc.vector.quantize_mx(out=g_codes[m][:, g, :].bitcast(FP8X4), scales=g_scales[m][:, g, :], in_=g_grouped[:])

        def pass2(acc, m, g, c0, width):
            cols = slice(c0, c0 + width)
            nc.tensor.matmul_mx(
                out=acc[:, 0:width],
                lhsT=g_codes[m][:, g, :].bitcast(FP8X4),
                lhsT_scale=g_scales[m][:, g, :],
                rhs=w2_words[:, g, cols].bitcast(FP8X4),
                rhs_scale=w2_planes[4 * g : P, cols],
                start=(g == 0),
                stop=(g == PASSES2 - 1),
            )

        def new_acc():
            acc = psum.tile([P, BANK], F32, tag="bank", name="acc2")
            return acc

        def finish(acc, m, c0, width):
            cols = slice(c0, c0 + width)
            result = stage.tile([P, BANK], F32, name="result", bufs=9)
            nc.vector.tensor_tensor(out=result[:, 0:width], in0=acc[:, 0:width], in1=b2_all[:, cols], op=ALU.add)
            nc.sync.dma_start(out=out[m * P : (m + 1) * P, cols], in_=result[:, 0:width])

        def layer2(m, c0, width):
            acc = new_acc()
            for g in range(PASSES2):
                pass2(acc, m, g, c0, width)
            finish(acc, m, c0, width)

        def layer1(m, c0, width, part):
            acc = passes1(m, c0, width)
            add_b1(acc, m, c0, width)
            square(m, c0, width, part)

        C0, C1, C2, C3 = (c * BANK for c in range(GROUPS))
        spread_copy(nc.scalar.copy, banks[0], 0, b1_all)
        spread_copy(nc.scalar.copy, banks[1], 1, b1_all)
        layer1(0, C0, BANK, 0)
        banks = [spread(sorted_rows[1], half) for half in range(2)]
        spread_copy(nc.scalar.copy, banks[0], 0, nw_all)
        spread_copy(nc.scalar.copy, banks[1], 1, nw_all)
        layer1(1, C0, BANK, 0)
        gain(nc.gpsimd, 0, 0)
        layer1(0, C1, BANK, 1)
        gain(nc.gpsimd, 0, 1)
        gain(nc.gpsimd, 1, 0)
        layer1(0, C2, BANK, 2)
        acc = passes1(1, C1, BANK)
        add_b1(acc, 1, C1, BANK)
        layer1(0, C3, HALF, 3)
        layer1(0, C3 + HALF, HALF, 4)
        square(1, C1, BANK, 1)
        gain(nc.vector, 0, 2)
        rstd0 = norm(0)
        for c0, part in ((C2, 2), (C3, 3)):
            acc = passes1(1, c0, BANK)
            add_b1(acc, 1, c0, BANK)
        rows0 = [silu(0, 0, rstd0, parts=2), silu(0, 1, rstd0)]
        square(1, C2, BANK, 2)
        rows0.append(silu(0, 2, rstd0))
        square(1, C3, BANK, 3)
        gain(nc.gpsimd, 0, 3)
        gain(nc.gpsimd, 1, 1)
        rows0.append(silu(0, 3, rstd0))
        accs = [new_acc() for n in range(CHUNKS2)]
        s_copy = nc.scalar.copy

        def block_a(g):
            for n in range(CHUNKS2):
                pass2(accs[n], 0, g, n * BANK, BANK)

        b2_banks = [spread(vec_rows[2], 0)]
        grouped0 = [g_turn(rows0[0])]
        g_quantise(0, 0, grouped0[0])
        b2_banks.append(spread(vec_rows[2], 1))
        grouped0.append(g_turn(rows0[1]))
        g_quantise(0, 1, grouped0[1])
        rstd1 = norm(1)
        for half in range(2):
            spread_copy(s_copy, b2_banks[half], half, b2_all)
        gain(nc.vector, 1, 2)
        block_a(0)
        grouped0.append(g_turn(rows0[2]))
        gain(nc.vector, 1, 3)
        g_quantise(0, 2, grouped0[2])
        block_a(1)
        grouped0.append(g_turn(rows0[3]))
        g_quantise(0, 3, grouped0[3])
        block_a(2)
        rows1 = [silu(1, g, rstd1) for g in range(GROUPS)]
        grouped1 = [g_turn(rows1[g], s_copy) for g in range(GROUPS)]
        block_a(3)
        for g in range(2):
            g_quantise(1, g, grouped1[g])
        finish(accs[0], 0, 0, BANK)
        for g in range(2, GROUPS):
            g_quantise(1, g, grouped1[g])
        for n in range(1, CHUNKS2):
            finish(accs[n], 0, n * BANK, BANK)
        for n in range(3):
            layer2(1, n * BANK, BANK)
        layer2(1, 3 * BANK, HALF)
        layer2(1, 3 * BANK + HALF, HALF)
